import numpy as np
import ml_dtypes


def mxq(x, axis, fmt="e4m3"):
    dtype, down = {"e4m3": (ml_dtypes.float8_e4m3fn, 7), "e5m2": (ml_dtypes.float8_e5m2, 14)}[fmt]
    v = np.moveaxis(np.asarray(x, np.float32).astype(ml_dtypes.bfloat16).astype(np.float64), axis, -1)
    blocks = v.reshape(v.shape[:-1] + (-1, 32))
    amax = np.abs(blocks).max(-1, keepdims=True)
    byte = np.maximum(np.where(amax > 0, np.frexp(amax)[1] - 1 + 127, 0) - down, 1)
    scale = np.exp2(byte - 127.0)
    codes = (blocks / scale).astype(np.float32).astype(dtype).astype(np.float64)
    return np.moveaxis((codes * scale).reshape(v.shape), -1, axis)


WIDE = False


def mx_kscale(k):
    if not WIDE:
        return np.ones(k)
    levels = np.array([10, -10, 5, -5, 0])
    a = np.random.permutation(np.resize(levels, k // 512 * 4)).reshape(k // 512, 4)
    idx = np.arange(k)
    return np.exp2(a[idx // 512, idx % 128 // 32])


BF16 = ml_dtypes.bfloat16


def bf(x):
    return np.asarray(x, np.float32).astype(BF16)


def f64(x):
    return np.asarray(x).astype(np.float64)


B, H, W, C, NH, KD = 10, 16, 32, 512, 4, 128
L = H * W
DV = C // NH
SCALE = 1.0 / np.sqrt(KD)


def rel_to_abs(r):
    b, n, w, _ = r.shape
    r = np.pad(r, ((0, 0), (0, 0), (0, 0), (0, 1)))
    r = r.reshape(b, n, w * 2 * w)
    r = np.pad(r, ((0, 0), (0, 0), (0, w - 1)))
    r = r.reshape(b, n, w + 1, 2 * w - 1)
    return r[:, :, :w, w - 1:]


def setup_inputs():
    s = mx_kscale(C)
    return {"q": bf(np.random.standard_normal((B, NH, L, KD))),
            "k": bf(np.random.standard_normal((B, NH, L, KD))),
            "x": bf(np.random.standard_normal((B, H, W, C)) * s),
            "w_v": bf(np.random.standard_normal((C, C)) * 2.0 / np.sqrt(C) / s[:, None]),
            "rel_w": bf(np.random.standard_normal((B, NH, H, W, 2 * W - 1))),
            "rel_h": bf(np.random.standard_normal((B, NH, W, H, 2 * H - 1)))}


def reference(q, k, x, w_v, rel_w, rel_h):
    v = mxq(f64(x).reshape(B, L, C), 2, "e4m3") @ mxq(f64(w_v), 0, "e4m3")
    v = v.reshape(B, L, NH, DV).transpose(0, 2, 1, 3)
    rw = rel_to_abs(f64(rel_w).reshape(B, NH * H, W, 2 * W - 1)).reshape(B, NH, H, W, W)
    rh = rel_to_abs(f64(rel_h).reshape(B, NH * W, H, 2 * H - 1)).reshape(B, NH, W, H, H)
    pos = rw[:, :, :, :, None, :] + rh.swapaxes(2, 3)[:, :, :, :, :, None]
    pos = pos.reshape(B, NH, L, L)
    sc = f64(q) @ f64(k).transpose(0, 1, 3, 2) * SCALE + pos
    e = np.exp(sc - sc.max(-1, keepdims=True))
    o = (mxq(e, 3, "e4m3") @ mxq(v, 2, "e4m3")) / e.sum(-1, keepdims=True)
    return o.transpose(0, 2, 1, 3).reshape(B, H, W, C)

@@ -1,0 +1,214 @@
+from contextlib import ExitStack
+import math
+
+import concourse.mybir as mybir
+from concourse.masks import make_identity
+
+F32 = mybir.dt.float32
+BF16 = mybir.dt.bfloat16
+U32 = mybir.dt.uint32
+U8 = mybir.dt.uint8
+FP8X4 = mybir.dt.float8_e4m3fn_x4
+ALU = mybir.AluOpType
+ACT = mybir.ActivationFunctionType
+
+B, GRID_H, GRID_W, C, NH, KD = 10, 16, 32, 512, 4, 128
+L = GRID_H * GRID_W
+P = 128
+PACK = 4
+LT = L // P
+ROWS_PER_TILE = P // GRID_W
+SCALE = 1.0 / math.sqrt(KD)
+REL_W = 2 * GRID_W - 1
+REL_H = 2 * GRID_H - 1
+RH_ROW_STEP = REL_H - 1
+RH_TILE_STEP = ROWS_PER_TILE * RH_ROW_STEP
+RH_RUN = (LT - 1) * RH_TILE_STEP + GRID_H
+
+FLOPS = 2 * B * L * C * C + 2 * 2 * B * NH * L * L * KD
+
+
+def tile_relativepositionmultiheadattention_pa_t_kernel(tc, q, k, x, w_v, rel_w, rel_h, out):
+    nc = tc.nc
+    with ExitStack() as ctx:
+        const = ctx.enter_context(tc.tile_pool(name="const", bufs=1))
+        loads = ctx.enter_context(tc.tile_pool(name="loads", bufs=2))
+        values = ctx.enter_context(tc.tile_pool(name="values", bufs=2))
+        heads = ctx.enter_context(tc.tile_pool(name="heads", bufs=2))
+        posp = ctx.enter_context(tc.tile_pool(name="posp", bufs=3))
+        work = ctx.enter_context(tc.tile_pool(name="work", bufs=4))
+        ps_sc = ctx.enter_context(tc.psum_pool(name="ps_sc", bufs=3))
+        ps_et = ctx.enter_context(tc.psum_pool(name="ps_et", bufs=2))
+        ps_o = ctx.enter_context(tc.psum_pool(name="ps_o", bufs=1))
+        ps_qk = ctx.enter_context(tc.psum_pool(name="ps_qk", bufs=1))
+        ps_v = ctx.enter_context(tc.psum_pool(name="ps_v", bufs=1))
+
+        ident_bf = const.tile([P, P], BF16)
+        make_identity(nc, ident_bf[:])
+        ident_f32 = const.tile([P, P], F32)
+        make_identity(nc, ident_f32[:])
+
+        w_sb = const.tile([P, 2, 2, C], BF16)
+        nc.sync.dma_start(out=w_sb[:], in_=w_v.rearrange("(u p e) n -> p u e n", u=2, e=2))
+        w_grouped = const.tile([P, C, PACK], BF16, align_bytes=64)
+        nc.vector.tensor_copy(out=w_grouped[:], in_=w_sb[:].rearrange("p u e n -> p n (u e)"))
+        w_codes = const.tile([P, C], U32, align_bytes=64)
+        w_scales = const.tile([P, C], U8, align_bytes=64)
+        nc.vector.quantize_mx(
+            out=w_codes[:].bitcast(FP8X4),
+            scales=w_scales[:],
+            in_=w_grouped[:].rearrange("p n t -> p (n t)"),
+        )
+
+        for b in range(B):
+            q_sb = loads.tile([P, NH * LT, KD], BF16)
+            nc.sync.dma_start(out=q_sb[:], in_=q[b].rearrange("n (j p) d -> p (n j) d", p=P))
+            k_sb = loads.tile([P, NH * LT, KD], BF16)
+            nc.sync.dma_start(out=k_sb[:], in_=k[b].rearrange("n (j p) d -> p (n j) d", p=P))
+            x_sb = loads.tile([P, LT, C], BF16)
+            nc.sync.dma_start(
+                out=x_sb[:], in_=x[b].rearrange("h w c -> (h w) c").rearrange("(t p) c -> p t c", p=P)
+            )
+            rw_sb = loads.tile([P, NH * LT, GRID_W], BF16)
+            rw_view = (
+                rel_w[b]
+                .rearrange("n r c m -> (n r) (c m)")[:, GRID_W - 1 : GRID_W - 1 + GRID_W * (REL_W - 1)]
+                .rearrange("a (c m) -> a c m", m=REL_W - 1)[:, :, 0:GRID_W]
+                .rearrange("(g s) c m -> s c g m", s=ROWS_PER_TILE)
+            )
+            rh_sb = loads.tile([P, NH, LT * RH_TILE_STEP], BF16)
+            rh_view = rel_h[b].rearrange("n c r m -> c n (r m)")
+            for s in range(ROWS_PER_TILE):
+                rows = slice(GRID_W * s, GRID_W * (s + 1))
+                nc.sync.dma_start(out=rw_sb[rows, :, :], in_=rw_view[s])
+                first = GRID_H - 1 + RH_ROW_STEP * s
+                nc.sync.dma_start(out=rh_sb[rows, :, 0:RH_RUN], in_=rh_view[:, :, first : first + RH_RUN])
+
+            x_words = x_sb[:].bitcast(F32)
+            x_grouped = values.tile([P, LT, P, PACK], BF16, align_bytes=64)
+            x_grouped_words = x_grouped[:].bitcast(F32)
+            for a in range(LT // 2):
+                xt_ps = ps_v.tile([P, 2, 2, P], F32, tag="v")
+                for i in range(2):
+                    for u in range(2):
+                        nc.tensor.transpose(
+                            xt_ps[:, i, u, :], x_words[:, 2 * a + i, P * u : P * (u + 1)], ident_f32[:]
+                        )
+                nc.scalar.copy(
+                    out=x_grouped_words[:, 2 * a : 2 * a + 2, :, :],
+                    in_=xt_ps[:].rearrange("p i u l -> p i l u"),
+                )
+            x_codes = values.tile([P, L], U32, align_bytes=64)
+            x_scales = values.tile([P, L], U8, align_bytes=64)
+            nc.vector.quantize_mx(
+                out=x_codes[:].bitcast(FP8X4),
+                scales=x_scales[:],
+                in_=x_grouped[:].rearrange("p t l w -> p (t l w)"),
+            )
+            v_grouped = values.tile([P, NH, KD, PACK], BF16, align_bytes=64)
+            for n in range(NH):
+                v_ps = ps_v.tile([P, LT, KD], F32, tag="v")
+                for t in range(LT):
+                    nc.tensor.matmul_mx(
+                        out=v_ps[:, t, :],
+                        lhsT=x_codes[:, P * t : P * (t + 1)].bitcast(FP8X4),
+                        lhsT_scale=x_scales[:, P * t : P * (t + 1)],
+                        rhs=w_codes[:, KD * n : KD * (n + 1)].bitcast(FP8X4),
+                        rhs_scale=w_scales[:, KD * n : KD * (n + 1)],
+                        start=True,
+                        stop=True,
+                    )
+                nc.scalar.copy(out=v_grouped[:, n, :, :], in_=v_ps[:].rearrange("p t d -> p d t"))
+            v_codes = values.tile([P, NH * KD], U32, align_bytes=64)
+            v_scales = values.tile([P, NH * KD], U8, align_bytes=64)
+            nc.vector.quantize_mx(
+                out=v_codes[:].bitcast(FP8X4),
+                scales=v_scales[:],
+                in_=v_grouped[:].rearrange("p n d t -> p (n d t)"),
+            )
+
+            o_sb = values.tile([P, LT, C], F32)
+            for n in range(NH):
+                pos = posp.tile([P, LT, GRID_H, GRID_W], F32)
+                nc.gpsimd.tensor_tensor(
+                    out=pos[:],
+                    in0=rw_sb[:, LT * n : LT * (n + 1), :].unsqueeze(2).to_broadcast([P, LT, GRID_H, GRID_W]),
+                    in1=rh_sb[:, n, :]
+                    .rearrange("p (j m) -> p j m", m=RH_TILE_STEP)[:, :, 0:GRID_H]
+                    .unsqueeze(3)
+                    .to_broadcast([P, LT, GRID_H, GRID_W]),
+                    op=ALU.add,
+                )
+                qk_ps = ps_qk.tile([P, 2, L], BF16)
+                for j in range(LT):
+                    nc.tensor.transpose(qk_ps[:, 0, P * j : P * (j + 1)], q_sb[:, LT * n + j, :], ident_bf[:])
+                for j in range(LT):
+                    nc.tensor.transpose(qk_ps[:, 1, P * j : P * (j + 1)], k_sb[:, LT * n + j, :], ident_bf[:])
+                qk_t = heads.tile([P, 2, L], BF16)
+                nc.scalar.copy(out=qk_t[:], in_=qk_ps[:])
+
+                neg_max = heads.tile([P, LT], F32)
+                row_sum = heads.tile([P, LT], F32)
+                e_codes = heads.tile([P, L], U32, align_bytes=64)
+                e_scales = heads.tile([P, L], U8, align_bytes=64)
+                for a in range(LT // 2):
+                    et_ps = ps_et.tile([P, 2, PACK, P], BF16)
+                    for i in range(2):
+                        j = 2 * a + i
+                        sc_ps = ps_sc.tile([P, L], F32)
+                        nc.tensor.matmul(
+                            sc_ps[:], lhsT=qk_t[:, 0, P * j : P * (j + 1)], rhs=qk_t[:, 1, :], start=True, stop=True
+                        )
+                        neg_s = work.tile([P, L], F32)
+                        nc.vector.scalar_tensor_tensor(
+                            out=neg_s[:],
+                            in0=sc_ps[:],
+                            scalar=-SCALE,
+                            in1=pos[:, j, :, :].rearrange("p r c -> p (r c)"),
+                            op0=ALU.mult,
+                            op1=ALU.subtract,
+                        )
+                        nc.vector.tensor_reduce(
+                            out=neg_max[:, j : j + 1], in_=neg_s[:], axis=mybir.AxisListType.X, op=ALU.min
+                        )
+                        e_sb = work.tile([P, L], BF16)
+                        nc.scalar.activation(
+                            out=e_sb[:],
+                            in_=neg_s[:],
+                            func=ACT.Exp,
+                            bias=neg_max[:, j : j + 1],
+                            scale=-1.0,
+                            accum_out=row_sum[:, j : j + 1],
+                        )
+                        for t in range(PACK):
+                            nc.tensor.transpose(et_ps[:, i, t, :], e_sb[:, P * t : P * (t + 1)], ident_bf[:])
+                    e_grouped = work.tile([P, 2, P, PACK], BF16, align_bytes=64)
+                    nc.scalar.copy(out=e_grouped[:], in_=et_ps[:].rearrange("p i t m -> p i m t"))
+                    cols = slice(2 * P * a, 2 * P * (a + 1))
+                    nc.vector.quantize_mx(
+                        out=e_codes[:, cols].bitcast(FP8X4),
+                        scales=e_scales[:, cols],
+                        in_=e_grouped[:].rearrange("p i m t -> p (i m t)"),
+                    )
+                o_ps = ps_o.tile([P, LT, KD], F32)
+                for j in range(LT):
+                    nc.tensor.matmul_mx(
+                        out=o_ps[:, j, :],
+                        lhsT=e_codes[:, P * j : P * (j + 1)].bitcast(FP8X4),
+                        lhsT_scale=e_scales[:, P * j : P * (j + 1)],
+                        rhs=v_codes[:, KD * n : KD * (n + 1)].bitcast(FP8X4),
+                        rhs_scale=v_scales[:, KD * n : KD * (n + 1)],
+                        start=True,
+                        stop=True,
+                    )
+                inv_sum = heads.tile([P, LT], F32)
+                nc.vector.reciprocal(out=inv_sum[:], in_=row_sum[:])
+                nc.vector.tensor_tensor(
+                    out=o_sb[:, :, KD * n : KD * (n + 1)],
+                    in0=o_ps[:],
+                    in1=inv_sum[:].unsqueeze(2).to_broadcast([P, LT, KD]),
+                    op=ALU.mult,
+                )
+            nc.sync.dma_start(
+                out=out[b].rearrange("h w c -> (h w) c").rearrange("(j p) c -> p j c", p=P), in_=o_sb[:]
+            )

@@ -130,15 +130,15 @@ def tile_relativepositionmultiheadattention_pa_t_kernel(tc, q, k, x, w_v, rel_w,
             o_sb = values.tile([P, LT, C], F32)
             for n in range(NH):
                 pos = posp.tile([P, LT, GRID_H, GRID_W], F32)
-                nc.gpsimd.tensor_tensor(
-                    out=pos[:],
-                    in0=rw_sb[:, LT * n : LT * (n + 1), :].unsqueeze(2).to_broadcast([P, LT, GRID_H, GRID_W]),
-                    in1=rh_sb[:, n, :]
-                    .rearrange("p (j m) -> p j m", m=RH_TILE_STEP)[:, :, 0:GRID_H]
-                    .unsqueeze(3)
-                    .to_broadcast([P, LT, GRID_H, GRID_W]),
-                    op=ALU.add,
-                )
+                for j in range(LT):
+                    nc.gpsimd.tensor_tensor(
+                        out=pos[:, j, :, :],
+                        in0=rw_sb[:, LT * n + j, :].unsqueeze(1).to_broadcast([P, GRID_H, GRID_W]),
+                        in1=rh_sb[:, n, RH_TILE_STEP * j : RH_TILE_STEP * j + GRID_H]
+                        .unsqueeze(2)
+                        .to_broadcast([P, GRID_H, GRID_W]),
+                        op=ALU.add,
+                    )
                 qk_ps = ps_qk.tile([P, 2, L], BF16)
                 for j in range(LT):
                     nc.tensor.transpose(qk_ps[:, 0, P * j : P * (j + 1)], q_sb[:, LT * n + j, :], ident_bf[:])

@@ -17,6 +17,8 @@ L = GRID_H * GRID_W
 P = 128
 PACK = 4
 LT = L // P
+HEADS = B * NH
+TILES = HEADS * LT
 ROWS_PER_TILE = P // GRID_W
 SCALE = 1.0 / math.sqrt(KD)
 REL_W = 2 * GRID_W - 1
@@ -32,183 +34,300 @@ def tile_relativepositionmultiheadattention_pa_t_kernel(tc, q, k, x, w_v, rel_w,
     nc = tc.nc
     with ExitStack() as ctx:
         const = ctx.enter_context(tc.tile_pool(name="const", bufs=1))
-        loads = ctx.enter_context(tc.tile_pool(name="loads", bufs=2))
-        values = ctx.enter_context(tc.tile_pool(name="values", bufs=2))
-        heads = ctx.enter_context(tc.tile_pool(name="heads", bufs=2))
-        posp = ctx.enter_context(tc.tile_pool(name="posp", bufs=3))
-        work = ctx.enter_context(tc.tile_pool(name="work", bufs=4))
-        ps_sc = ctx.enter_context(tc.psum_pool(name="ps_sc", bufs=3))
-        ps_et = ctx.enter_context(tc.psum_pool(name="ps_et", bufs=2))
-        ps_o = ctx.enter_context(tc.psum_pool(name="ps_o", bufs=1))
-        ps_qk = ctx.enter_context(tc.psum_pool(name="ps_qk", bufs=1))
-        ps_v = ctx.enter_context(tc.psum_pool(name="ps_v", bufs=1))
+        loads = ctx.enter_context(tc.tile_pool(name="loads", bufs=3))
 
         ident_bf = const.tile([P, P], BF16)
         make_identity(nc, ident_bf[:])
         ident_f32 = const.tile([P, P], F32)
         make_identity(nc, ident_f32[:])
 
-        w_sb = const.tile([P, 2, 2, C], BF16)
-        nc.sync.dma_start(out=w_sb[:], in_=w_v.rearrange("(u p e) n -> p u e n", u=2, e=2))
-        w_grouped = const.tile([P, C, PACK], BF16, align_bytes=64)
-        nc.vector.tensor_copy(out=w_grouped[:], in_=w_sb[:].rearrange("p u e n -> p n (u e)"))
-        w_codes = const.tile([P, C], U32, align_bytes=64)
-        w_scales = const.tile([P, C], U8, align_bytes=64)
-        nc.vector.quantize_mx(
-            out=w_codes[:].bitcast(FP8X4),
-            scales=w_scales[:],
-            in_=w_grouped[:].rearrange("p n t -> p (n t)"),
-        )
+        q_sb, k_sb, rw_sb, rh_sb = {}, {}, {}, {}
 
-        for b in range(B):
-            q_sb = loads.tile([P, NH * LT, KD], BF16)
-            nc.sync.dma_start(out=q_sb[:], in_=q[b].rearrange("n (j p) d -> p (n j) d", p=P))
-            k_sb = loads.tile([P, NH * LT, KD], BF16)
-            nc.sync.dma_start(out=k_sb[:], in_=k[b].rearrange("n (j p) d -> p (n j) d", p=P))
-            x_sb = loads.tile([P, LT, C], BF16)
-            nc.sync.dma_start(
-                out=x_sb[:], in_=x[b].rearrange("h w c -> (h w) c").rearrange("(t p) c -> p t c", p=P)
-            )
-            rw_sb = loads.tile([P, NH * LT, GRID_W], BF16)
+        def load_bias_tables(b):
+            rw = loads.tile([P, NH * LT, GRID_W], BF16)
             rw_view = (
                 rel_w[b]
                 .rearrange("n r c m -> (n r) (c m)")[:, GRID_W - 1 : GRID_W - 1 + GRID_W * (REL_W - 1)]
                 .rearrange("a (c m) -> a c m", m=REL_W - 1)[:, :, 0:GRID_W]
                 .rearrange("(g s) c m -> s c g m", s=ROWS_PER_TILE)
             )
-            rh_sb = loads.tile([P, NH, LT * RH_TILE_STEP], BF16)
+            rh = loads.tile([P, NH, LT * RH_TILE_STEP], BF16)
             rh_view = rel_h[b].rearrange("n c r m -> c n (r m)")
             for s in range(ROWS_PER_TILE):
                 rows = slice(GRID_W * s, GRID_W * (s + 1))
-                nc.sync.dma_start(out=rw_sb[rows, :, :], in_=rw_view[s])
+                nc.sync.dma_start(out=rw[rows, :, :], in_=rw_view[s])
                 first = GRID_H - 1 + RH_ROW_STEP * s
-                nc.sync.dma_start(out=rh_sb[rows, :, 0:RH_RUN], in_=rh_view[:, :, first : first + RH_RUN])
+                nc.sync.dma_start(out=rh[rows, :, 0:RH_RUN], in_=rh_view[:, :, first : first + RH_RUN])
+            rw_sb[b], rh_sb[b] = rw, rh
 
-            x_words = x_sb[:].bitcast(F32)
-            x_grouped = values.tile([P, LT, P, PACK], BF16, align_bytes=64)
-            x_grouped_words = x_grouped[:].bitcast(F32)
-            for a in range(LT // 2):
-                xt_ps = ps_v.tile([P, 2, 2, P], F32, tag="v")
-                for i in range(2):
-                    for u in range(2):
-                        nc.tensor.transpose(
-                            xt_ps[:, i, u, :], x_words[:, 2 * a + i, P * u : P * (u + 1)], ident_f32[:]
-                        )
-                nc.scalar.copy(
-                    out=x_grouped_words[:, 2 * a : 2 * a + 2, :, :],
-                    in_=xt_ps[:].rearrange("p i u l -> p i l u"),
+        def load_queries_and_keys(b):
+            q_tile = loads.tile([P, NH * LT, KD], BF16)
+            nc.sync.dma_start(out=q_tile[:], in_=q[b].rearrange("n (j p) d -> p (n j) d", p=P))
+            k_tile = loads.tile([P, NH * LT, KD], BF16)
+            nc.sync.dma_start(out=k_tile[:], in_=k[b].rearrange("n (j p) d -> p (n j) d", p=P))
+            q_sb[b], k_sb[b] = q_tile, k_tile
+
+        v_codes = const.tile([P, B, NH * KD], U32, align_bytes=64)
+        v_scales = const.tile([P, B, NH * KD], U8, align_bytes=64)
+        with ExitStack() as phase1:
+            stage = phase1.enter_context(tc.tile_pool(name="stage", bufs=3))
+            ps_x = phase1.enter_context(tc.psum_pool(name="ps_x", bufs=2))
+            ps_v = phase1.enter_context(tc.psum_pool(name="ps_v", bufs=4))
+
+            w_sb = const.tile([P, 2, 2, C], BF16)
+            nc.sync.dma_start(out=w_sb[:], in_=w_v.rearrange("(u p e) n -> p u e n", u=2, e=2))
+            w_grouped = const.tile([P, C, PACK], BF16, align_bytes=64)
+            nc.vector.tensor_copy(out=w_grouped[:], in_=w_sb[:].rearrange("p u e n -> p n (u e)"))
+            w_codes = const.tile([P, C], U32, align_bytes=64)
+            w_scales = const.tile([P, C], U8, align_bytes=64)
+            nc.vector.quantize_mx(
+                out=w_codes[:].bitcast(FP8X4),
+                scales=w_scales[:],
+                in_=w_grouped[:].rearrange("p n t -> p (n t)"),
+            )
+
+            for b in range(B):
+                x_sb = stage.tile([P, LT, C], BF16)
+                nc.sync.dma_start(
+                    out=x_sb[:], in_=x[b].rearrange("h w c -> (h w) c").rearrange("(t p) c -> p t c", p=P)
                 )
-            x_codes = values.tile([P, L], U32, align_bytes=64)
-            x_scales = values.tile([P, L], U8, align_bytes=64)
-            nc.vector.quantize_mx(
-                out=x_codes[:].bitcast(FP8X4),
-                scales=x_scales[:],
-                in_=x_grouped[:].rearrange("p t l w -> p (t l w)"),
-            )
-            v_grouped = values.tile([P, NH, KD, PACK], BF16, align_bytes=64)
-            for n in range(NH):
-                v_ps = ps_v.tile([P, LT, KD], F32, tag="v")
-                for t in range(LT):
-                    nc.tensor.matmul_mx(
-                        out=v_ps[:, t, :],
-                        lhsT=x_codes[:, P * t : P * (t + 1)].bitcast(FP8X4),
-                        lhsT_scale=x_scales[:, P * t : P * (t + 1)],
-                        rhs=w_codes[:, KD * n : KD * (n + 1)].bitcast(FP8X4),
-                        rhs_scale=w_scales[:, KD * n : KD * (n + 1)],
-                        start=True,
-                        stop=True,
-                    )
-                nc.scalar.copy(out=v_grouped[:, n, :, :], in_=v_ps[:].rearrange("p t d -> p d t"))
-            v_codes = values.tile([P, NH * KD], U32, align_bytes=64)
-            v_scales = values.tile([P, NH * KD], U8, align_bytes=64)
-            nc.vector.quantize_mx(
-                out=v_codes[:].bitcast(FP8X4),
-                scales=v_scales[:],
-                in_=v_grouped[:].rearrange("p n d t -> p (n d t)"),
-            )
-
-            o_sb = values.tile([P, LT, C], F32)
-            for n in range(NH):
-                pos = posp.tile([P, LT, GRID_H, GRID_W], F32)
-                for j in range(LT):
-                    nc.gpsimd.tensor_tensor(
-                        out=pos[:, j, :, :],
-                        in0=rw_sb[:, LT * n + j, :].unsqueeze(1).to_broadcast([P, GRID_H, GRID_W]),
-                        in1=rh_sb[:, n, RH_TILE_STEP * j : RH_TILE_STEP * j + GRID_H]
-                        .unsqueeze(2)
-                        .to_broadcast([P, GRID_H, GRID_W]),
-                        op=ALU.add,
-                    )
-                qk_ps = ps_qk.tile([P, 2, L], BF16)
-                for j in range(LT):
-                    nc.tensor.transpose(qk_ps[:, 0, P * j : P * (j + 1)], q_sb[:, LT * n + j, :], ident_bf[:])
-                for j in range(LT):
-                    nc.tensor.transpose(qk_ps[:, 1, P * j : P * (j + 1)], k_sb[:, LT * n + j, :], ident_bf[:])
-                qk_t = heads.tile([P, 2, L], BF16)
-                nc.scalar.copy(out=qk_t[:], in_=qk_ps[:])
-
-                neg_max = heads.tile([P, LT], F32)
-                row_sum = heads.tile([P, LT], F32)
-                e_codes = heads.tile([P, L], U32, align_bytes=64)
-                e_scales = heads.tile([P, L], U8, align_bytes=64)
+                if b == 0:
+                    load_bias_tables(0)
+                x_words = x_sb[:].bitcast(F32)
+                x_grouped = stage.tile([P, LT, P, PACK], BF16, align_bytes=64)
+                x_grouped_words = x_grouped[:].bitcast(F32)
                 for a in range(LT // 2):
-                    et_ps = ps_et.tile([P, 2, PACK, P], BF16)
+                    xt_ps = ps_x.tile([P, 2, 2, P], F32)
                     for i in range(2):
-                        j = 2 * a + i
-                        sc_ps = ps_sc.tile([P, L], F32)
-                        nc.tensor.matmul(
-                            sc_ps[:], lhsT=qk_t[:, 0, P * j : P * (j + 1)], rhs=qk_t[:, 1, :], start=True, stop=True
-                        )
-                        neg_s = work.tile([P, L], F32)
-                        nc.vector.scalar_tensor_tensor(
-                            out=neg_s[:],
-                            in0=sc_ps[:],
-                            scalar=-SCALE,
-                            in1=pos[:, j, :, :].rearrange("p r c -> p (r c)"),
-                            op0=ALU.mult,
-                            op1=ALU.subtract,
-                        )
-                        nc.vector.tensor_reduce(
-                            out=neg_max[:, j : j + 1], in_=neg_s[:], axis=mybir.AxisListType.X, op=ALU.min
-                        )
-                        e_sb = work.tile([P, L], BF16)
-                        nc.scalar.activation(
-                            out=e_sb[:],
-                            in_=neg_s[:],
-                            func=ACT.Exp,
-                            bias=neg_max[:, j : j + 1],
-                            scale=-1.0,
-                            accum_out=row_sum[:, j : j + 1],
-                        )
-                        for t in range(PACK):
-                            nc.tensor.transpose(et_ps[:, i, t, :], e_sb[:, P * t : P * (t + 1)], ident_bf[:])
-                    e_grouped = work.tile([P, 2, P, PACK], BF16, align_bytes=64)
-                    nc.scalar.copy(out=e_grouped[:], in_=et_ps[:].rearrange("p i t m -> p i m t"))
-                    cols = slice(2 * P * a, 2 * P * (a + 1))
-                    nc.vector.quantize_mx(
-                        out=e_codes[:, cols].bitcast(FP8X4),
-                        scales=e_scales[:, cols],
-                        in_=e_grouped[:].rearrange("p i m t -> p (i m t)"),
+                        for u in range(2):
+                            nc.tensor.transpose(
+                                xt_ps[:, i, u, :], x_words[:, 2 * a + i, P * u : P * (u + 1)], ident_f32[:]
+                            )
+                    copy_out = nc.scalar.copy if a == 0 else nc.vector.tensor_copy
+                    copy_out(
+                        out=x_grouped_words[:, 2 * a : 2 * a + 2, :, :],
+                        in_=xt_ps[:].rearrange("p i u l -> p i l u"),
                     )
-                o_ps = ps_o.tile([P, LT, KD], F32)
-                for j in range(LT):
-                    nc.tensor.matmul_mx(
-                        out=o_ps[:, j, :],
-                        lhsT=e_codes[:, P * j : P * (j + 1)].bitcast(FP8X4),
-                        lhsT_scale=e_scales[:, P * j : P * (j + 1)],
-                        rhs=v_codes[:, KD * n : KD * (n + 1)].bitcast(FP8X4),
-                        rhs_scale=v_scales[:, KD * n : KD * (n + 1)],
-                        start=True,
-                        stop=True,
-                    )
-                inv_sum = heads.tile([P, LT], F32)
-                nc.vector.reciprocal(out=inv_sum[:], in_=row_sum[:])
-                nc.vector.tensor_tensor(
-                    out=o_sb[:, :, KD * n : KD * (n + 1)],
-                    in0=o_ps[:],
-                    in1=inv_sum[:].unsqueeze(2).to_broadcast([P, LT, KD]),
-                    op=ALU.mult,
+                x_codes = stage.tile([P, L], U32, align_bytes=64)
+                x_scales = stage.tile([P, L], U8, align_bytes=64)
+                nc.vector.quantize_mx(
+                    out=x_codes[:].bitcast(FP8X4),
+                    scales=x_scales[:],
+                    in_=x_grouped[:].rearrange("p t l w -> p (t l w)"),
                 )
-            nc.sync.dma_start(
-                out=out[b].rearrange("h w c -> (h w) c").rearrange("(j p) c -> p j c", p=P), in_=o_sb[:]
+                v_grouped = stage.tile([P, NH, KD, PACK], BF16, align_bytes=64)
+                for n in range(NH):
+                    v_ps = ps_v.tile([P, LT, KD], F32)
+                    for t in range(LT):
+                        nc.tensor.matmul_mx(
+                            out=v_ps[:, t, :],
+                            lhsT=x_codes[:, P * t : P * (t + 1)].bitcast(FP8X4),
+                            lhsT_scale=x_scales[:, P * t : P * (t + 1)],
+                            rhs=w_codes[:, KD * n : KD * (n + 1)].bitcast(FP8X4),
+                            rhs_scale=w_scales[:, KD * n : KD * (n + 1)],
+                            start=True,
+                            stop=True,
+                        )
+                    copy_out = nc.vector.tensor_copy if n == 0 else nc.scalar.copy
+                    copy_out(out=v_grouped[:, n, :, :], in_=v_ps[:].rearrange("p t d -> p d t"))
+                nc.vector.quantize_mx(
+                    out=v_codes[:, b, :].bitcast(FP8X4),
+                    scales=v_scales[:, b, :],
+                    in_=v_grouped[:].rearrange("p n d t -> p (n d t)"),
+                )
+            load_queries_and_keys(0)
+            load_bias_tables(1)
+            load_queries_and_keys(1)
+
+        heads = ctx.enter_context(tc.tile_pool(name="heads", bufs=2))
+        stats = ctx.enter_context(tc.tile_pool(name="stats", bufs=3))
+        grouped = ctx.enter_context(tc.tile_pool(name="grouped", bufs=3))
+        work = ctx.enter_context(tc.tile_pool(name="work", bufs=4))
+        ps_sc = ctx.enter_context(tc.psum_pool(name="ps_sc", bufs=4))
+        ps_et = ctx.enter_context(tc.psum_pool(name="ps_et", bufs=2))
+        ps_o = ctx.enter_context(tc.psum_pool(name="ps_o", bufs=1))
+        ps_qk = ctx.enter_context(tc.psum_pool(name="ps_qk", bufs=1))
+
+        pos, qk_ps, qk_t, neg_max, row_sum, inv_sum = {}, {}, {}, {}, {}, {}
+        e_grouped, e_codes, e_scales, o_sb = {}, {}, {}, {}
+        sc_ps, neg_s, e_sb, et_ps = {}, {}, {}, {}
+
+        def position_bias(h):
+            if not 0 <= h < HEADS:
+                return
+            b, n = divmod(h, NH)
+            pos_tile = heads.tile([P, LT, GRID_H, GRID_W], F32)
+            nc.gpsimd.tensor_tensor(
+                out=pos_tile[:],
+                in0=rw_sb[b][:, LT * n : LT * (n + 1), :].unsqueeze(2).to_broadcast([P, LT, GRID_H, GRID_W]),
+                in1=rh_sb[b][:, n, :]
+                .rearrange("p (j m) -> p j m", m=RH_TILE_STEP)[:, :, 0:GRID_H]
+                .unsqueeze(3)
+                .to_broadcast([P, LT, GRID_H, GRID_W]),
+                op=ALU.add,
             )
+            pos[h] = pos_tile
+
+        def transpose_qk(h):
+            if not 0 <= h < HEADS:
+                return
+            b, n = divmod(h, NH)
+            qk_bank = ps_qk.tile([P, 2, L], BF16)
+            for j in range(LT):
+                nc.tensor.transpose(qk_bank[:, 0, P * j : P * (j + 1)], q_sb[b][:, LT * n + j, :], ident_bf[:])
+            for j in range(LT):
+                nc.tensor.transpose(qk_bank[:, 1, P * j : P * (j + 1)], k_sb[b][:, LT * n + j, :], ident_bf[:])
+            qk_ps[h] = qk_bank
+
+        def copy_qk(h):
+            if not 0 <= h < HEADS:
+                return
+            qk_tile = heads.tile([P, 2, L], BF16)
+            nc.scalar.copy(out=qk_tile[:], in_=qk_ps[h][:])
+            qk_t[h] = qk_tile
+
+        def scores_matmul(i):
+            if not 0 <= i < TILES:
+                return
+            h, j = divmod(i, LT)
+            sc_bank = ps_sc.tile([P, L], F32)
+            nc.tensor.matmul(
+                sc_bank[:], lhsT=qk_t[h][:, 0, P * j : P * (j + 1)], rhs=qk_t[h][:, 1, :], start=True, stop=True
+            )
+            sc_ps[i] = sc_bank
+
+        def add_bias(i):
+            if not 0 <= i < TILES:
+                return
+            h, j = divmod(i, LT)
+            neg_s_tile = work.tile([P, L], F32)
+            nc.vector.scalar_tensor_tensor(
+                out=neg_s_tile[:],
+                in0=sc_ps[i][:],
+                scalar=-SCALE,
+                in1=pos[h][:, j, :, :].rearrange("p r c -> p (r c)"),
+                op0=ALU.mult,
+                op1=ALU.subtract,
+            )
+            neg_s[i] = neg_s_tile
+
+        def row_minimum(i):
+            if not 0 <= i < TILES:
+                return
+            h, j = divmod(i, LT)
+            if j == 0:
+                neg_max_tile = stats.tile([P, LT], F32)
+                neg_max[h] = neg_max_tile
+            nc.vector.tensor_reduce(
+                out=neg_max[h][:, j : j + 1], in_=neg_s[i][:], axis=mybir.AxisListType.X, op=ALU.min
+            )
+
+        def exponent(i):
+            if not 0 <= i < TILES:
+                return
+            h, j = divmod(i, LT)
+            if j == 0:
+                row_sum_tile = stats.tile([P, LT], F32)
+                row_sum[h] = row_sum_tile
+            e_tile = work.tile([P, L], BF16)
+            nc.scalar.activation(
+                out=e_tile[:],
+                in_=neg_s[i][:],
+                func=ACT.Exp,
+                bias=neg_max[h][:, j : j + 1],
+                scale=-1.0,
+                accum_out=row_sum[h][:, j : j + 1],
+            )
+            e_sb[i] = e_tile
+
+        def transpose_e(i):
+            if not 0 <= i < TILES:
+                return
+            et_bank = ps_et.tile([P, PACK, P], BF16)
+            for t in range(PACK):
+                nc.tensor.transpose(et_bank[:, t, :], e_sb[i][:, P * t : P * (t + 1)], ident_bf[:])
+            et_ps[i] = et_bank
+
+        def copy_e(i):
+            if not 0 <= i < TILES:
+                return
+            h, j = divmod(i, LT)
+            if j == 0:
+                e_grouped_tile = grouped.tile([P, LT, P, PACK], BF16, align_bytes=64)
+                e_grouped[h] = e_grouped_tile
+            nc.scalar.copy(out=e_grouped[h][:, j, :, :], in_=et_ps[i][:].rearrange("p t m -> p m t"))
+
+        def quantise_e(h):
+            if not 0 <= h < HEADS:
+                return
+            e_codes_tile = heads.tile([P, L], U32, align_bytes=64)
+            e_scales_tile = heads.tile([P, L], U8, align_bytes=64)
+            nc.vector.quantize_mx(
+                out=e_codes_tile[:].bitcast(FP8X4),
+                scales=e_scales_tile[:],
+                in_=e_grouped[h][:].rearrange("p j m t -> p (j m t)"),
+            )
+            inv_sum_tile = stats.tile([P, LT], F32)
+            nc.vector.reciprocal(out=inv_sum_tile[:], in_=row_sum[h][:])
+            e_codes[h], e_scales[h], inv_sum[h] = e_codes_tile, e_scales_tile, inv_sum_tile
+
+        o_ps = {}
+
+        def output_matmul(h):
+            if not 0 <= h < HEADS:
+                return
+            b, n = divmod(h, NH)
+            o_bank = ps_o.tile([P, LT, KD], F32)
+            for j in range(LT):
+                nc.tensor.matmul_mx(
+                    out=o_bank[:, j, :],
+                    lhsT=e_codes[h][:, P * j : P * (j + 1)].bitcast(FP8X4),
+                    lhsT_scale=e_scales[h][:, P * j : P * (j + 1)],
+                    rhs=v_codes[:, b, KD * n : KD * (n + 1)].bitcast(FP8X4),
+                    rhs_scale=v_scales[:, b, KD * n : KD * (n + 1)],
+                    start=True,
+                    stop=True,
+                )
+            o_ps[h] = o_bank
+
+        def normalise(h):
+            if not 0 <= h < HEADS:
+                return
+            b, n = divmod(h, NH)
+            if n == 0:
+                o_tile = heads.tile([P, LT, C], F32)
+                o_sb[b] = o_tile
+            nc.vector.tensor_tensor(
+                out=o_sb[b][:, :, KD * n : KD * (n + 1)],
+                in0=o_ps[h][:],
+                in1=inv_sum[h][:].unsqueeze(2).to_broadcast([P, LT, KD]),
+                op=ALU.mult,
+            )
+            if n == NH - 1:
+                nc.sync.dma_start(
+                    out=out[b].rearrange("h w c -> (h w) c").rearrange("(j p) c -> p j c", p=P), in_=o_sb[b][:]
+                )
+
+        with tc.manual_schedule():
+            for i in range(-7, LT * (HEADS + 2) - 1):
+                h, j = divmod(i, LT)
+                if i >= 0 and i % (NH * LT) == 0 and h // NH + 2 < B:
+                    load_bias_tables(h // NH + 2)
+                    load_queries_and_keys(h // NH + 2)
+                if j == 1:
+                    transpose_qk(h + 2)
+                scores_matmul(i + 4)
+                if j == 1:
+                    quantise_e(h - 2)
+                add_bias(i + 2)
+                if j == 1:
+                    position_bias(h + 2)
+                row_minimum(i + 1)
+                exponent(i)
+                if j == 1:
+                    output_matmul(h - 2)
+                transpose_e(i)
+                copy_e(i - 1)
+                if j == 2:
+                    copy_qk(h + 2)
+                    normalise(h - 2)

@@ -317,10 +317,9 @@ def tile_relativepositionmultiheadattention_pa_t_kernel(tc, q, k, x, w_v, rel_w,
                 if j == 1:
                     transpose_qk(h + 2)
                 scores_matmul(i + 4)
-                if j == 1:
-                    quantise_e(h - 2)
                 add_bias(i + 2)
                 if j == 1:
+                    quantise_e(h - 2)
                     position_bias(h + 2)
                 row_minimum(i + 1)
                 exponent(i)

@@ -27,6 +27,8 @@ RH_ROW_STEP = REL_H - 1
 RH_TILE_STEP = ROWS_PER_TILE * RH_ROW_STEP
 RH_RUN = (LT - 1) * RH_TILE_STEP + GRID_H
 
+X_BUFS = 4
+
 FLOPS = 2 * B * L * C * C + 2 * 2 * B * NH * L * L * KD
 
 
@@ -35,13 +37,23 @@ def tile_relativepositionmultiheadattention_pa_t_kernel(tc, q, k, x, w_v, rel_w,
     with ExitStack() as ctx:
         const = ctx.enter_context(tc.tile_pool(name="const", bufs=1))
         loads = ctx.enter_context(tc.tile_pool(name="loads", bufs=3))
+        x_pool = ctx.enter_context(tc.tile_pool(name="x_pool", bufs=X_BUFS))
+        stage = ctx.enter_context(tc.tile_pool(name="stage", bufs=2))
+        heads = ctx.enter_context(tc.tile_pool(name="heads", bufs=2))
+        stats = ctx.enter_context(tc.tile_pool(name="stats", bufs=3))
+        grouped = ctx.enter_context(tc.tile_pool(name="grouped", bufs=3))
+        work = ctx.enter_context(tc.tile_pool(name="work", bufs=4))
+        ps_sc = ctx.enter_context(tc.psum_pool(name="ps_sc", bufs=4))
+        ps_et = ctx.enter_context(tc.psum_pool(name="ps_et", bufs=2))
+        ps_o = ctx.enter_context(tc.psum_pool(name="ps_o", bufs=1))
+        ps_qk = ctx.enter_context(tc.psum_pool(name="ps_qk", bufs=1))
 
         ident_bf = const.tile([P, P], BF16)
         make_identity(nc, ident_bf[:])
         ident_f32 = const.tile([P, P], F32)
         make_identity(nc, ident_f32[:])
 
-        q_sb, k_sb, rw_sb, rh_sb = {}, {}, {}, {}
+        q_sb, k_sb, rw_sb, rh_sb, x_sb = {}, {}, {}, {}, {}
 
         def load_bias_tables(b):
             rw = loads.tile([P, NH * LT, GRID_W], BF16)
@@ -67,89 +79,105 @@ def tile_relativepositionmultiheadattention_pa_t_kernel(tc, q, k, x, w_v, rel_w,
             nc.sync.dma_start(out=k_tile[:], in_=k[b].rearrange("n (j p) d -> p (n j) d", p=P))
             q_sb[b], k_sb[b] = q_tile, k_tile
 
+        def load_x(b):
+            if not 0 <= b < B:
+                return
+            x_tile = x_pool.tile([P, LT, C], BF16)
+            nc.sync.dma_start(
+                out=x_tile[:], in_=x[b].rearrange("h w c -> (h w) c").rearrange("(t p) c -> p t c", p=P)
+            )
+            x_sb[b] = x_tile
+
         v_codes = const.tile([P, B, NH * KD], U32, align_bytes=64)
         v_scales = const.tile([P, B, NH * KD], U8, align_bytes=64)
-        with ExitStack() as phase1:
-            stage = phase1.enter_context(tc.tile_pool(name="stage", bufs=3))
-            ps_x = phase1.enter_context(tc.psum_pool(name="ps_x", bufs=2))
-            ps_v = phase1.enter_context(tc.psum_pool(name="ps_v", bufs=4))
+        w_codes = const.tile([P, C], U32, align_bytes=64)
+        w_scales = const.tile([P, C], U8, align_bytes=64)
+        xt_ps, x_grouped, x_codes, x_scales, v_ps, v_grouped = {}, {}, {}, {}, {}, {}
 
+        def quantise_w():
             w_sb = const.tile([P, 2, 2, C], BF16)
             nc.sync.dma_start(out=w_sb[:], in_=w_v.rearrange("(u p e) n -> p u e n", u=2, e=2))
             w_grouped = const.tile([P, C, PACK], BF16, align_bytes=64)
             nc.vector.tensor_copy(out=w_grouped[:], in_=w_sb[:].rearrange("p u e n -> p n (u e)"))
-            w_codes = const.tile([P, C], U32, align_bytes=64)
-            w_scales = const.tile([P, C], U8, align_bytes=64)
             nc.vector.quantize_mx(
                 out=w_codes[:].bitcast(FP8X4),
                 scales=w_scales[:],
                 in_=w_grouped[:].rearrange("p n t -> p (n t)"),
             )
 
-            for b in range(B):
-                x_sb = stage.tile([P, LT, C], BF16)
-                nc.sync.dma_start(
-                    out=x_sb[:], in_=x[b].rearrange("h w c -> (h w) c").rearrange("(t p) c -> p t c", p=P)
-                )
-                if b == 0:
-                    load_bias_tables(0)
-                x_words = x_sb[:].bitcast(F32)
-                x_grouped = stage.tile([P, LT, P, PACK], BF16, align_bytes=64)
-                x_grouped_words = x_grouped[:].bitcast(F32)
-                for a in range(LT // 2):
-                    xt_ps = ps_x.tile([P, 2, 2, P], F32)
-                    for i in range(2):
-                        for u in range(2):
-                            nc.tensor.transpose(
-                                xt_ps[:, i, u, :], x_words[:, 2 * a + i, P * u : P * (u + 1)], ident_f32[:]
-                            )
-                    copy_out = nc.scalar.copy if a == 0 else nc.vector.tensor_copy
-                    copy_out(
-                        out=x_grouped_words[:, 2 * a : 2 * a + 2, :, :],
-                        in_=xt_ps[:].rearrange("p i u l -> p i l u"),
-                    )
-                x_codes = stage.tile([P, L], U32, align_bytes=64)
-                x_scales = stage.tile([P, L], U8, align_bytes=64)
-                nc.vector.quantize_mx(
-                    out=x_codes[:].bitcast(FP8X4),
-                    scales=x_scales[:],
-                    in_=x_grouped[:].rearrange("p t l w -> p (t l w)"),
-                )
-                v_grouped = stage.tile([P, NH, KD, PACK], BF16, align_bytes=64)
-                for n in range(NH):
-                    v_ps = ps_v.tile([P, LT, KD], F32)
-                    for t in range(LT):
-                        nc.tensor.matmul_mx(
-                            out=v_ps[:, t, :],
-                            lhsT=x_codes[:, P * t : P * (t + 1)].bitcast(FP8X4),
-                            lhsT_scale=x_scales[:, P * t : P * (t + 1)],
-                            rhs=w_codes[:, KD * n : KD * (n + 1)].bitcast(FP8X4),
-                            rhs_scale=w_scales[:, KD * n : KD * (n + 1)],
-                            start=True,
-                            stop=True,
+        def transpose_x(b):
+            if not 0 <= b < B:
+                return
+            x_words = x_sb[b][:].bitcast(F32)
+            for a in range(LT // 2):
+                xt_bank = ps_et.tile([P, 2, 2, P], F32, tag="et")
+                for i in range(2):
+                    for u in range(2):
+                        nc.tensor.transpose(
+                            xt_bank[:, i, u, :], x_words[:, 2 * a + i, P * u : P * (u + 1)], ident_f32[:]
                         )
-                    copy_out = nc.vector.tensor_copy if n == 0 else nc.scalar.copy
-                    copy_out(out=v_grouped[:, n, :, :], in_=v_ps[:].rearrange("p t d -> p d t"))
-                nc.vector.quantize_mx(
-                    out=v_codes[:, b, :].bitcast(FP8X4),
-                    scales=v_scales[:, b, :],
-                    in_=v_grouped[:].rearrange("p n d t -> p (n d t)"),
-                )
-            load_queries_and_keys(0)
-            load_bias_tables(1)
-            load_queries_and_keys(1)
+                xt_ps[b, a] = xt_bank
 
-        heads = ctx.enter_context(tc.tile_pool(name="heads", bufs=2))
-        stats = ctx.enter_context(tc.tile_pool(name="stats", bufs=3))
-        grouped = ctx.enter_context(tc.tile_pool(name="grouped", bufs=3))
-        work = ctx.enter_context(tc.tile_pool(name="work", bufs=4))
-        ps_sc = ctx.enter_context(tc.psum_pool(name="ps_sc", bufs=4))
-        ps_et = ctx.enter_context(tc.psum_pool(name="ps_et", bufs=2))
-        ps_o = ctx.enter_context(tc.psum_pool(name="ps_o", bufs=1))
-        ps_qk = ctx.enter_context(tc.psum_pool(name="ps_qk", bufs=1))
+        def copy_x(b):
+            if not 0 <= b < B:
+                return
+            x_grouped_tile = stage.tile([P, LT, P, PACK], BF16, align_bytes=64)
+            x_grouped_words = x_grouped_tile[:].bitcast(F32)
+            nc.scalar.copy(out=x_grouped_words[:, 0:2, :, :], in_=xt_ps[b, 0][:].rearrange("p i u l -> p i l u"))
+            nc.vector.tensor_copy(
+                out=x_grouped_words[:, 2:4, :, :], in_=xt_ps[b, 1][:].rearrange("p i u l -> p i l u")
+            )
+            x_grouped[b] = x_grouped_tile
+
+        def quantise_x(b):
+            if not 0 <= b < B:
+                return
+            x_codes_tile = stage.tile([P, L], U32, align_bytes=64)
+            x_scales_tile = stage.tile([P, L], U8, align_bytes=64)
+            nc.vector.quantize_mx(
+                out=x_codes_tile[:].bitcast(FP8X4),
+                scales=x_scales_tile[:],
+                in_=x_grouped[b][:].rearrange("p t l w -> p (t l w)"),
+            )
+            x_codes[b], x_scales[b] = x_codes_tile, x_scales_tile
+
+        def value_matmul(b):
+            if not 0 <= b < B:
+                return
+            for n in range(NH):
+                v_bank = ps_sc.tile([P, LT, KD], F32, tag="sc")
+                for t in range(LT):
+                    nc.tensor.matmul_mx(
+                        out=v_bank[:, t, :],
+                        lhsT=x_codes[b][:, P * t : P * (t + 1)].bitcast(FP8X4),
+                        lhsT_scale=x_scales[b][:, P * t : P * (t + 1)],
+                        rhs=w_codes[:, KD * n : KD * (n + 1)].bitcast(FP8X4),
+                        rhs_scale=w_scales[:, KD * n : KD * (n + 1)],
+                        start=True,
+                        stop=True,
+                    )
+                v_ps[b, n] = v_bank
+
+        def copy_v(b):
+            if not 0 <= b < B:
+                return
+            v_grouped_tile = stage.tile([P, NH, KD, PACK], BF16, align_bytes=64)
+            nc.vector.tensor_copy(out=v_grouped_tile[:, 0, :, :], in_=v_ps[b, 0][:].rearrange("p t d -> p d t"))
+            for n in range(1, NH):
+                nc.scalar.copy(out=v_grouped_tile[:, n, :, :], in_=v_ps[b, n][:].rearrange("p t d -> p d t"))
+            v_grouped[b] = v_grouped_tile
+
+        def quantise_v(b):
+            if not 0 <= b < B:
+                return
+            nc.vector.quantize_mx(
+                out=v_codes[:, b, :].bitcast(FP8X4),
+                scales=v_scales[:, b, :],
+                in_=v_grouped[b][:].rearrange("p n d t -> p (n d t)"),
+            )
 
         pos, qk_ps, qk_t, neg_max, row_sum, inv_sum = {}, {}, {}, {}, {}, {}
-        e_grouped, e_codes, e_scales, o_sb = {}, {}, {}, {}
+        e_grouped, e_codes, e_scales = {}, {}, {}
         sc_ps, neg_s, e_sb, et_ps = {}, {}, {}, {}
 
         def position_bias(h):
@@ -190,7 +218,7 @@ def tile_relativepositionmultiheadattention_pa_t_kernel(tc, q, k, x, w_v, rel_w,
             if not 0 <= i < TILES:
                 return
             h, j = divmod(i, LT)
-            sc_bank = ps_sc.tile([P, L], F32)
+            sc_bank = ps_sc.tile([P, L], F32, tag="sc")
             nc.tensor.matmul(
                 sc_bank[:], lhsT=qk_t[h][:, 0, P * j : P * (j + 1)], rhs=qk_t[h][:, 1, :], start=True, stop=True
             )
@@ -243,7 +271,7 @@ def tile_relativepositionmultiheadattention_pa_t_kernel(tc, q, k, x, w_v, rel_w,
         def transpose_e(i):
             if not 0 <= i < TILES:
                 return
-            et_bank = ps_et.tile([P, PACK, P], BF16)
+            et_bank = ps_et.tile([P, PACK, P], BF16, tag="et")
             for t in range(PACK):
                 nc.tensor.transpose(et_bank[:, t, :], e_sb[i][:, P * t : P * (t + 1)], ident_bf[:])
             et_ps[i] = et_bank
@@ -294,22 +322,44 @@ def tile_relativepositionmultiheadattention_pa_t_kernel(tc, q, k, x, w_v, rel_w,
             if not 0 <= h < HEADS:
                 return
             b, n = divmod(h, NH)
-            if n == 0:
-                o_tile = heads.tile([P, LT, C], F32)
-                o_sb[b] = o_tile
-            nc.vector.tensor_tensor(
-                out=o_sb[b][:, :, KD * n : KD * (n + 1)],
-                in0=o_ps[h][:],
-                in1=inv_sum[h][:].unsqueeze(2).to_broadcast([P, LT, KD]),
-                op=ALU.mult,
-            )
-            if n == NH - 1:
-                nc.sync.dma_start(
-                    out=out[b].rearrange("h w c -> (h w) c").rearrange("(j p) c -> p j c", p=P), in_=o_sb[b][:]
+            o_tile = heads.tile([P, LT, KD], F32)
+            if h % 2 == 0:
+                for j in range(LT):
+                    nc.scalar.activation(
+                        out=o_tile[:, j, :], in_=o_ps[h][:, j, :], func=ACT.Copy, scale=inv_sum[h][:, j : j + 1]
+                    )
+            else:
+                nc.vector.tensor_tensor(
+                    out=o_tile[:],
+                    in0=o_ps[h][:],
+                    in1=inv_sum[h][:].unsqueeze(2).to_broadcast([P, LT, KD]),
+                    op=ALU.mult,
                 )
+            nc.sync.dma_start(
+                out=out[b].rearrange("h w c -> (h w) c").rearrange("(j p) c -> p j c", p=P)[
+                    :, :, KD * n : KD * (n + 1)
+                ],
+                in_=o_tile[:],
+            )
 
         with tc.manual_schedule():
-            for i in range(-7, LT * (HEADS + 2) - 1):
+            quantise_w()
+            load_x(0)
+            load_bias_tables(0)
+            for b in range(1, X_BUFS):
+                load_x(b)
+            for b in range(-1, B):
+                transpose_x(b + 1)
+                load_x(b + 1 + X_BUFS)
+                copy_x(b + 1)
+                value_matmul(b)
+                copy_v(b)
+                quantise_x(b + 1)
+                quantise_v(b)
+            load_queries_and_keys(0)
+            load_bias_tables(1)
+            load_queries_and_keys(1)
+            for i in range(-7, LT * (HEADS + 2)):
                 h, j = divmod(i, LT)
                 if i >= 0 and i % (NH * LT) == 0 and h // NH + 2 < B:
                     load_bias_tables(h // NH + 2)
@@ -329,4 +379,5 @@ def tile_relativepositionmultiheadattention_pa_t_kernel(tc, q, k, x, w_v, rel_w,
                 copy_e(i - 1)
                 if j == 2:
                     copy_qk(h + 2)
+                if j == 3:
                     normalise(h - 2)

@@ -92,7 +92,7 @@ def tile_relativepositionmultiheadattention_pa_t_kernel(tc, q, k, x, w_v, rel_w,
         v_scales = const.tile([P, B, NH * KD], U8, align_bytes=64)
         w_codes = const.tile([P, C], U32, align_bytes=64)
         w_scales = const.tile([P, C], U8, align_bytes=64)
-        xt_ps, x_grouped, x_codes, x_scales, v_ps, v_grouped = {}, {}, {}, {}, {}, {}
+        xt_ps, x_grouped, x_codes, x_scales, v_grouped = {}, {}, {}, {}, {}
 
         def quantise_w():
             w_sb = const.tile([P, 2, 2, C], BF16)
@@ -144,6 +144,7 @@ def tile_relativepositionmultiheadattention_pa_t_kernel(tc, q, k, x, w_v, rel_w,
         def value_matmul(b):
             if not 0 <= b < B:
                 return
+            v_grouped_tile = stage.tile([P, NH, KD, PACK], BF16, align_bytes=64)
             for n in range(NH):
                 v_bank = ps_sc.tile([P, LT, KD], F32, tag="sc")
                 for t in range(LT):
@@ -156,15 +157,8 @@ def tile_relativepositionmultiheadattention_pa_t_kernel(tc, q, k, x, w_v, rel_w,
                         start=True,
                         stop=True,
                     )
-                v_ps[b, n] = v_bank
-
-        def copy_v(b):
-            if not 0 <= b < B:
-                return
-            v_grouped_tile = stage.tile([P, NH, KD, PACK], BF16, align_bytes=64)
-            nc.vector.tensor_copy(out=v_grouped_tile[:, 0, :, :], in_=v_ps[b, 0][:].rearrange("p t d -> p d t"))
-            for n in range(1, NH):
-                nc.scalar.copy(out=v_grouped_tile[:, n, :, :], in_=v_ps[b, n][:].rearrange("p t d -> p d t"))
+                copy_out = nc.vector.tensor_copy if n == 0 else nc.scalar.copy
+                copy_out(out=v_grouped_tile[:, n, :, :], in_=v_bank[:].rearrange("p t d -> p d t"))
             v_grouped[b] = v_grouped_tile
 
         def quantise_v(b):
@@ -211,7 +205,8 @@ def tile_relativepositionmultiheadattention_pa_t_kernel(tc, q, k, x, w_v, rel_w,
             if not 0 <= h < HEADS:
                 return
             qk_tile = heads.tile([P, 2, L], BF16)
-            nc.scalar.copy(out=qk_tile[:], in_=qk_ps[h][:])
+            copy_out = nc.scalar.copy if h % NH == 0 else nc.vector.tensor_copy
+            copy_out(out=qk_tile[:], in_=qk_ps[h][:])
             qk_t[h] = qk_tile
 
         def scores_matmul(i):
@@ -323,17 +318,9 @@ def tile_relativepositionmultiheadattention_pa_t_kernel(tc, q, k, x, w_v, rel_w,
                 return
             b, n = divmod(h, NH)
             o_tile = heads.tile([P, LT, KD], F32)
-            if h % 2 == 0:
-                for j in range(LT):
-                    nc.scalar.activation(
-                        out=o_tile[:, j, :], in_=o_ps[h][:, j, :], func=ACT.Copy, scale=inv_sum[h][:, j : j + 1]
-                    )
-            else:
-                nc.vector.tensor_tensor(
-                    out=o_tile[:],
-                    in0=o_ps[h][:],
-                    in1=inv_sum[h][:].unsqueeze(2).to_broadcast([P, LT, KD]),
-                    op=ALU.mult,
+            for j in range(LT):
+                nc.scalar.activation(
+                    out=o_tile[:, j, :], in_=o_ps[h][:, j, :], func=ACT.Copy, scale=inv_sum[h][:, j : j + 1]
                 )
             nc.sync.dma_start(
                 out=out[b].rearrange("h w c -> (h w) c").rearrange("(j p) c -> p j c", p=P)[
@@ -353,18 +340,17 @@ def tile_relativepositionmultiheadattention_pa_t_kernel(tc, q, k, x, w_v, rel_w,
                 load_x(b + 1 + X_BUFS)
                 copy_x(b + 1)
                 value_matmul(b)
-                copy_v(b)
                 quantise_x(b + 1)
                 quantise_v(b)
             load_queries_and_keys(0)
             load_bias_tables(1)
             load_queries_and_keys(1)
-            for i in range(-7, LT * (HEADS + 2)):
+            for i in range(-8, LT * (HEADS + 2)):
                 h, j = divmod(i, LT)
                 if i >= 0 and i % (NH * LT) == 0 and h // NH + 2 < B:
                     load_bias_tables(h // NH + 2)
                     load_queries_and_keys(h // NH + 2)
-                if j == 1:
+                if j == 0:
                     transpose_qk(h + 2)
                 scores_matmul(i + 4)
                 add_bias(i + 2)

@@ -84,7 +84,8 @@ def tile_relativepositionmultiheadattention_pa_t_kernel(tc, q, k, x, w_v, rel_w,
                 return
             x_tile = x_pool.tile([P, LT, C], BF16)
             nc.sync.dma_start(
-                out=x_tile[:], in_=x[b].rearrange("h w c -> (h w) c").rearrange("(t p) c -> p t c", p=P)
+                out=x_tile[:].rearrange("p (u e) c -> p u e c", e=2),
+                in_=x[b].rearrange("h w c -> (h w) c").rearrange("(u p e) c -> p u e c", p=P, e=2)
             )
             x_sb[b] = x_tile
 
@@ -266,9 +267,10 @@ def tile_relativepositionmultiheadattention_pa_t_kernel(tc, q, k, x, w_v, rel_w,
         def transpose_e(i):
             if not 0 <= i < TILES:
                 return
-            et_bank = ps_et.tile([P, PACK, P], BF16, tag="et")
-            for t in range(PACK):
-                nc.tensor.transpose(et_bank[:, t, :], e_sb[i][:, P * t : P * (t + 1)], ident_bf[:])
+            e_words = e_sb[i][:].bitcast(F32)
+            et_bank = ps_et.tile([P, 2, P], F32, tag="et")
+            for u in range(2):
+                nc.tensor.transpose(et_bank[:, u, :], e_words[:, P * u : P * (u + 1)], ident_f32[:])
             et_ps[i] = et_bank
 
         def copy_e(i):
@@ -278,7 +280,7 @@ def tile_relativepositionmultiheadattention_pa_t_kernel(tc, q, k, x, w_v, rel_w,
             if j == 0:
                 e_grouped_tile = grouped.tile([P, LT, P, PACK], BF16, align_bytes=64)
                 e_grouped[h] = e_grouped_tile
-            nc.scalar.copy(out=e_grouped[h][:, j, :, :], in_=et_ps[i][:].rearrange("p t m -> p m t"))
+            nc.scalar.copy(out=e_grouped[h][:].bitcast(F32)[:, j, :, :], in_=et_ps[i][:].rearrange("p u m -> p m u"))
 
         def quantise_e(h):
             if not 0 <= h < HEADS:

@@ -27,8 +27,6 @@ RH_ROW_STEP = REL_H - 1
 RH_TILE_STEP = ROWS_PER_TILE * RH_ROW_STEP
 RH_RUN = (LT - 1) * RH_TILE_STEP + GRID_H
 
-X_BUFS = 4
-
 FLOPS = 2 * B * L * C * C + 2 * 2 * B * NH * L * L * KD
 
 
@@ -37,14 +35,16 @@ def tile_relativepositionmultiheadattention_pa_t_kernel(tc, q, k, x, w_v, rel_w,
     with ExitStack() as ctx:
         const = ctx.enter_context(tc.tile_pool(name="const", bufs=1))
         loads = ctx.enter_context(tc.tile_pool(name="loads", bufs=3))
-        x_pool = ctx.enter_context(tc.tile_pool(name="x_pool", bufs=X_BUFS))
+        x_pool = ctx.enter_context(tc.tile_pool(name="x_pool", bufs=3))
         stage = ctx.enter_context(tc.tile_pool(name="stage", bufs=2))
+        biases = ctx.enter_context(tc.tile_pool(name="biases", bufs=3))
         heads = ctx.enter_context(tc.tile_pool(name="heads", bufs=2))
         stats = ctx.enter_context(tc.tile_pool(name="stats", bufs=3))
         grouped = ctx.enter_context(tc.tile_pool(name="grouped", bufs=3))
-        work = ctx.enter_context(tc.tile_pool(name="work", bufs=4))
-        ps_sc = ctx.enter_context(tc.psum_pool(name="ps_sc", bufs=4))
+        work = ctx.enter_context(tc.tile_pool(name="work", bufs=6))
+        ps_sc = ctx.enter_context(tc.psum_pool(name="ps_sc", bufs=3))
         ps_et = ctx.enter_context(tc.psum_pool(name="ps_et", bufs=2))
+        ps_val = ctx.enter_context(tc.psum_pool(name="ps_val", bufs=1))
         ps_o = ctx.enter_context(tc.psum_pool(name="ps_o", bufs=1))
         ps_qk = ctx.enter_context(tc.psum_pool(name="ps_qk", bufs=1))
 
@@ -56,6 +56,8 @@ def tile_relativepositionmultiheadattention_pa_t_kernel(tc, q, k, x, w_v, rel_w,
         q_sb, k_sb, rw_sb, rh_sb, x_sb = {}, {}, {}, {}, {}
 
         def load_bias_tables(b):
+            if not 0 <= b < B:
+                return
             rw = loads.tile([P, NH * LT, GRID_W], BF16)
             rw_view = (
                 rel_w[b]
@@ -72,12 +74,18 @@ def tile_relativepositionmultiheadattention_pa_t_kernel(tc, q, k, x, w_v, rel_w,
                 nc.sync.dma_start(out=rh[rows, :, 0:RH_RUN], in_=rh_view[:, :, first : first + RH_RUN])
             rw_sb[b], rh_sb[b] = rw, rh
 
-        def load_queries_and_keys(b):
-            q_tile = loads.tile([P, NH * LT, KD], BF16)
-            nc.sync.dma_start(out=q_tile[:], in_=q[b].rearrange("n (j p) d -> p (n j) d", p=P))
-            k_tile = loads.tile([P, NH * LT, KD], BF16)
-            nc.sync.dma_start(out=k_tile[:], in_=k[b].rearrange("n (j p) d -> p (n j) d", p=P))
-            q_sb[b], k_sb[b] = q_tile, k_tile
+        def load_queries_and_keys(b, first_head=0, last_head=NH):
+            if not 0 <= b < B:
+                return
+            if first_head == 0:
+                q_tile = loads.tile([P, NH * LT, KD], BF16)
+                k_tile = loads.tile([P, NH * LT, KD], BF16)
+                q_sb[b], k_sb[b] = q_tile, k_tile
+            tiles = slice(LT * first_head, LT * last_head)
+            q_view = q[b].rearrange("n (j p) d -> p (n j) d", p=P)
+            k_view = k[b].rearrange("n (j p) d -> p (n j) d", p=P)
+            nc.sync.dma_start(out=q_sb[b][:, tiles, :], in_=q_view[:, tiles, :])
+            nc.sync.dma_start(out=k_sb[b][:, tiles, :], in_=k_view[:, tiles, :])
 
         def load_x(b):
             if not 0 <= b < B:
@@ -85,19 +93,19 @@ def tile_relativepositionmultiheadattention_pa_t_kernel(tc, q, k, x, w_v, rel_w,
             x_tile = x_pool.tile([P, LT, C], BF16)
             nc.sync.dma_start(
                 out=x_tile[:].rearrange("p (u e) c -> p u e c", e=2),
-                in_=x[b].rearrange("h w c -> (h w) c").rearrange("(u p e) c -> p u e c", p=P, e=2)
+                in_=x[b].rearrange("h w c -> (h w) c").rearrange("(u p e) c -> p u e c", p=P, e=2),
             )
             x_sb[b] = x_tile
 
-        v_codes = const.tile([P, B, NH * KD], U32, align_bytes=64)
-        v_scales = const.tile([P, B, NH * KD], U8, align_bytes=64)
         w_codes = const.tile([P, C], U32, align_bytes=64)
         w_scales = const.tile([P, C], U8, align_bytes=64)
-        xt_ps, x_grouped, x_codes, x_scales, v_grouped = {}, {}, {}, {}, {}
+        w_sb = const.tile([P, 2, 2, C], BF16)
+        val_ps, x_grouped, x_codes, x_scales, v_grouped, v_codes, v_scales = {}, {}, {}, {}, {}, {}, {}
+
+        def load_w():
+            nc.sync.dma_start(out=w_sb[:], in_=w_v.rearrange("(u p e) n -> p u e n", u=2, e=2))
 
         def quantise_w():
-            w_sb = const.tile([P, 2, 2, C], BF16)
-            nc.sync.dma_start(out=w_sb[:], in_=w_v.rearrange("(u p e) n -> p u e n", u=2, e=2))
             w_grouped = const.tile([P, C, PACK], BF16, align_bytes=64)
             nc.vector.tensor_copy(out=w_grouped[:], in_=w_sb[:].rearrange("p u e n -> p n (u e)"))
             nc.vector.quantize_mx(
@@ -106,33 +114,26 @@ def tile_relativepositionmultiheadattention_pa_t_kernel(tc, q, k, x, w_v, rel_w,
                 in_=w_grouped[:].rearrange("p n t -> p (n t)"),
             )
 
-        def transpose_x(b):
-            if not 0 <= b < B:
-                return
+        def transpose_x(b, a):
             x_words = x_sb[b][:].bitcast(F32)
-            for a in range(LT // 2):
-                xt_bank = ps_et.tile([P, 2, 2, P], F32, tag="et")
-                for i in range(2):
-                    for u in range(2):
-                        nc.tensor.transpose(
-                            xt_bank[:, i, u, :], x_words[:, 2 * a + i, P * u : P * (u + 1)], ident_f32[:]
-                        )
-                xt_ps[b, a] = xt_bank
+            xt_bank = ps_val.tile([P, 2, 2, P], F32, tag="val")
+            for i in range(2):
+                for u in range(2):
+                    nc.tensor.transpose(
+                        xt_bank[:, i, u, :], x_words[:, 2 * a + i, P * u : P * (u + 1)], ident_f32[:]
+                    )
+            val_ps[b] = xt_bank
 
-        def copy_x(b):
-            if not 0 <= b < B:
-                return
-            x_grouped_tile = stage.tile([P, LT, P, PACK], BF16, align_bytes=64)
-            x_grouped_words = x_grouped_tile[:].bitcast(F32)
-            nc.scalar.copy(out=x_grouped_words[:, 0:2, :, :], in_=xt_ps[b, 0][:].rearrange("p i u l -> p i l u"))
-            nc.vector.tensor_copy(
-                out=x_grouped_words[:, 2:4, :, :], in_=xt_ps[b, 1][:].rearrange("p i u l -> p i l u")
+        def copy_x(b, a):
+            if a == 0:
+                x_grouped_tile = stage.tile([P, LT, P, PACK], BF16, align_bytes=64)
+                x_grouped[b] = x_grouped_tile
+            nc.scalar.copy(
+                out=x_grouped[b][:].bitcast(F32)[:, 2 * a : 2 * a + 2, :, :],
+                in_=val_ps[b][:].rearrange("p i u l -> p i l u"),
             )
-            x_grouped[b] = x_grouped_tile
 
         def quantise_x(b):
-            if not 0 <= b < B:
-                return
             x_codes_tile = stage.tile([P, L], U32, align_bytes=64)
             x_scales_tile = stage.tile([P, L], U8, align_bytes=64)
             nc.vector.quantize_mx(
@@ -142,34 +143,36 @@ def tile_relativepositionmultiheadattention_pa_t_kernel(tc, q, k, x, w_v, rel_w,
             )
             x_codes[b], x_scales[b] = x_codes_tile, x_scales_tile
 
-        def value_matmul(b):
-            if not 0 <= b < B:
-                return
-            v_grouped_tile = stage.tile([P, NH, KD, PACK], BF16, align_bytes=64)
-            for n in range(NH):
-                v_bank = ps_sc.tile([P, LT, KD], F32, tag="sc")
-                for t in range(LT):
-                    nc.tensor.matmul_mx(
-                        out=v_bank[:, t, :],
-                        lhsT=x_codes[b][:, P * t : P * (t + 1)].bitcast(FP8X4),
-                        lhsT_scale=x_scales[b][:, P * t : P * (t + 1)],
-                        rhs=w_codes[:, KD * n : KD * (n + 1)].bitcast(FP8X4),
-                        rhs_scale=w_scales[:, KD * n : KD * (n + 1)],
-                        start=True,
-                        stop=True,
-                    )
-                copy_out = nc.vector.tensor_copy if n == 0 else nc.scalar.copy
-                copy_out(out=v_grouped_tile[:, n, :, :], in_=v_bank[:].rearrange("p t d -> p d t"))
-            v_grouped[b] = v_grouped_tile
+        def value_matmul(b, n):
+            v_bank = ps_val.tile([P, LT, KD], F32, tag="val")
+            for t in range(LT):
+                nc.tensor.matmul_mx(
+                    out=v_bank[:, t, :],
+                    lhsT=x_codes[b][:, P * t : P * (t + 1)].bitcast(FP8X4),
+                    lhsT_scale=x_scales[b][:, P * t : P * (t + 1)],
+                    rhs=w_codes[:, KD * n : KD * (n + 1)].bitcast(FP8X4),
+                    rhs_scale=w_scales[:, KD * n : KD * (n + 1)],
+                    start=True,
+                    stop=True,
+                )
+            val_ps[b] = v_bank
+
+        def copy_v(b, n):
+            if n == 0:
+                v_grouped_tile = stage.tile([P, NH, KD, PACK], BF16, align_bytes=64)
+                v_grouped[b] = v_grouped_tile
+            copy_out = nc.vector.tensor_copy if n == 0 else nc.scalar.copy
+            copy_out(out=v_grouped[b][:, n, :, :], in_=val_ps[b][:].rearrange("p t d -> p d t"))
 
         def quantise_v(b):
-            if not 0 <= b < B:
-                return
+            v_codes_tile = stage.tile([P, NH * KD], U32, align_bytes=64)
+            v_scales_tile = stage.tile([P, NH * KD], U8, align_bytes=64)
             nc.vector.quantize_mx(
-                out=v_codes[:, b, :].bitcast(FP8X4),
-                scales=v_scales[:, b, :],
+                out=v_codes_tile[:].bitcast(FP8X4),
+                scales=v_scales_tile[:],
                 in_=v_grouped[b][:].rearrange("p n d t -> p (n d t)"),
             )
+            v_codes[b], v_scales[b] = v_codes_tile, v_scales_tile
 
         pos, qk_ps, qk_t, neg_max, row_sum, inv_sum = {}, {}, {}, {}, {}, {}
         e_grouped, e_codes, e_scales = {}, {}, {}
@@ -179,16 +182,20 @@ def tile_relativepositionmultiheadattention_pa_t_kernel(tc, q, k, x, w_v, rel_w,
             if not 0 <= h < HEADS:
                 return
             b, n = divmod(h, NH)
-            pos_tile = heads.tile([P, LT, GRID_H, GRID_W], F32)
-            nc.gpsimd.tensor_tensor(
-                out=pos_tile[:],
-                in0=rw_sb[b][:, LT * n : LT * (n + 1), :].unsqueeze(2).to_broadcast([P, LT, GRID_H, GRID_W]),
-                in1=rh_sb[b][:, n, :]
-                .rearrange("p (j m) -> p j m", m=RH_TILE_STEP)[:, :, 0:GRID_H]
-                .unsqueeze(3)
-                .to_broadcast([P, LT, GRID_H, GRID_W]),
-                op=ALU.add,
-            )
+            pos_tile = biases.tile([P, LT, GRID_H, GRID_W], F32)
+            width = 1 if h == 0 else LT
+            for j in range(0, LT, width):
+                nc.gpsimd.tensor_tensor(
+                    out=pos_tile[:, j : j + width, :, :],
+                    in0=rw_sb[b][:, LT * n + j : LT * n + j + width, :]
+                    .unsqueeze(2)
+                    .to_broadcast([P, width, GRID_H, GRID_W]),
+                    in1=rh_sb[b][:, n, :]
+                    .rearrange("p (j m) -> p j m", m=RH_TILE_STEP)[:, j : j + width, 0:GRID_H]
+                    .unsqueeze(3)
+                    .to_broadcast([P, width, GRID_H, GRID_W]),
+                    op=ALU.add,
+                )
             pos[h] = pos_tile
 
         def transpose_qk(h):
@@ -206,8 +213,7 @@ def tile_relativepositionmultiheadattention_pa_t_kernel(tc, q, k, x, w_v, rel_w,
             if not 0 <= h < HEADS:
                 return
             qk_tile = heads.tile([P, 2, L], BF16)
-            copy_out = nc.scalar.copy if h % NH == 0 else nc.vector.tensor_copy
-            copy_out(out=qk_tile[:], in_=qk_ps[h][:])
+            nc.scalar.copy(out=qk_tile[:].bitcast(F32), in_=qk_ps[h][:].bitcast(F32))
             qk_t[h] = qk_tile
 
         def scores_matmul(i):
@@ -308,8 +314,8 @@ def tile_relativepositionmultiheadattention_pa_t_kernel(tc, q, k, x, w_v, rel_w,
                     out=o_bank[:, j, :],
                     lhsT=e_codes[h][:, P * j : P * (j + 1)].bitcast(FP8X4),
                     lhsT_scale=e_scales[h][:, P * j : P * (j + 1)],
-                    rhs=v_codes[:, b, KD * n : KD * (n + 1)].bitcast(FP8X4),
-                    rhs_scale=v_scales[:, b, KD * n : KD * (n + 1)],
+                    rhs=v_codes[b][:, KD * n : KD * (n + 1)].bitcast(FP8X4),
+                    rhs_scale=v_scales[b][:, KD * n : KD * (n + 1)],
                     start=True,
                     stop=True,
                 )
@@ -332,39 +338,49 @@ def tile_relativepositionmultiheadattention_pa_t_kernel(tc, q, k, x, w_v, rel_w,
             )
 
         with tc.manual_schedule():
-            quantise_w()
-            load_x(0)
+            load_queries_and_keys(0, 0, 1)
             load_bias_tables(0)
-            for b in range(1, X_BUFS):
-                load_x(b)
-            for b in range(-1, B):
-                transpose_x(b + 1)
-                load_x(b + 1 + X_BUFS)
-                copy_x(b + 1)
-                value_matmul(b)
-                quantise_x(b + 1)
-                quantise_v(b)
-            load_queries_and_keys(0)
+            load_w()
+            load_x(0)
+            load_queries_and_keys(0, 1, NH)
+            load_x(1)
             load_bias_tables(1)
             load_queries_and_keys(1)
-            for i in range(-8, LT * (HEADS + 2)):
+            quantise_w()
+            for i in range(-12, LT * (HEADS + 2)):
                 h, j = divmod(i, LT)
-                if i >= 0 and i % (NH * LT) == 0 and h // NH + 2 < B:
+                vb, r = divmod(i + 4, LT * NH)
+                make_values = 0 <= vb < B
+                if i >= 0 and i % (NH * LT) == 0:
+                    load_x(h // NH + 2)
                     load_bias_tables(h // NH + 2)
                     load_queries_and_keys(h // NH + 2)
                 if j == 0:
                     transpose_qk(h + 2)
-                scores_matmul(i + 4)
-                add_bias(i + 2)
-                if j == 1:
+                scores_matmul(i + 5)
+                add_bias(i + 3)
+                if j == 0:
                     quantise_e(h - 2)
-                    position_bias(h + 2)
-                row_minimum(i + 1)
+                    if make_values and r == 4:
+                        quantise_x(vb)
+                    if make_values and r == 12:
+                        quantise_v(vb)
+                    position_bias(h + 3)
+                row_minimum(i + 2)
                 exponent(i)
-                if j == 1:
+                if j == 0:
                     output_matmul(h - 2)
                 transpose_e(i)
                 copy_e(i - 1)
+                if make_values:
+                    if r in (1, 2):
+                        copy_x(vb, r - 1)
+                    if r in (0, 1):
+                        transpose_x(vb, r)
+                    if r in (6, 7, 8, 9):
+                        copy_v(vb, r - 6)
+                    if r in (5, 6, 7, 8):
+                        value_matmul(vb, r - 5)
                 if j == 2:
                     copy_qk(h + 2)
                 if j == 3:

@@ -27,6 +27,24 @@ RH_ROW_STEP = REL_H - 1
 RH_TILE_STEP = ROWS_PER_TILE * RH_ROW_STEP
 RH_RUN = (LT - 1) * RH_TILE_STEP + GRID_H
 
+BIAS_HEADS = tuple(h for h in range(HEADS) if h % 3 != 0)
+BIAS_TILE = 0
+BIAS_COLS = P // 2
+
+SC = 5
+TE = 1
+CE = 2
+TX = (1, 3)
+VM = (9, 11, 13, 15)
+VC = (10, 12, 14, 16)
+QX = 8
+QV = 4
+AD = 3
+MN = 2
+CEF = False
+VV = (0,)
+OJ = 1
+NORM = (2, 3)
 FLOPS = 2 * B * L * C * C + 2 * 2 * B * NH * L * L * KD
 
 
@@ -39,7 +57,7 @@ def tile_relativepositionmultiheadattention_pa_t_kernel(tc, q, k, x, w_v, rel_w,
         stage = ctx.enter_context(tc.tile_pool(name="stage", bufs=2))
         biases = ctx.enter_context(tc.tile_pool(name="biases", bufs=3))
         heads = ctx.enter_context(tc.tile_pool(name="heads", bufs=2))
-        stats = ctx.enter_context(tc.tile_pool(name="stats", bufs=3))
+        stats = ctx.enter_context(tc.tile_pool(name="stats", bufs=8))
         grouped = ctx.enter_context(tc.tile_pool(name="grouped", bufs=3))
         work = ctx.enter_context(tc.tile_pool(name="work", bufs=6))
         ps_sc = ctx.enter_context(tc.psum_pool(name="ps_sc", bufs=3))
@@ -107,7 +125,7 @@ def tile_relativepositionmultiheadattention_pa_t_kernel(tc, q, k, x, w_v, rel_w,
 
         def quantise_w():
             w_grouped = const.tile([P, C, PACK], BF16, align_bytes=64)
-            nc.vector.tensor_copy(out=w_grouped[:], in_=w_sb[:].rearrange("p u e n -> p n (u e)"))
+            nc.scalar.copy(out=w_grouped[:], in_=w_sb[:].rearrange("p u e n -> p n (u e)"))
             nc.vector.quantize_mx(
                 out=w_codes[:].bitcast(FP8X4),
                 scales=w_scales[:],
@@ -115,6 +133,8 @@ def tile_relativepositionmultiheadattention_pa_t_kernel(tc, q, k, x, w_v, rel_w,
             )
 
         def transpose_x(b, a):
+            if not 0 <= b < B:
+                return
             x_words = x_sb[b][:].bitcast(F32)
             xt_bank = ps_val.tile([P, 2, 2, P], F32, tag="val")
             for i in range(2):
@@ -125,6 +145,8 @@ def tile_relativepositionmultiheadattention_pa_t_kernel(tc, q, k, x, w_v, rel_w,
             val_ps[b] = xt_bank
 
         def copy_x(b, a):
+            if not 0 <= b < B:
+                return
             if a == 0:
                 x_grouped_tile = stage.tile([P, LT, P, PACK], BF16, align_bytes=64)
                 x_grouped[b] = x_grouped_tile
@@ -134,6 +156,8 @@ def tile_relativepositionmultiheadattention_pa_t_kernel(tc, q, k, x, w_v, rel_w,
             )
 
         def quantise_x(b):
+            if not 0 <= b < B:
+                return
             x_codes_tile = stage.tile([P, L], U32, align_bytes=64)
             x_scales_tile = stage.tile([P, L], U8, align_bytes=64)
             nc.vector.quantize_mx(
@@ -144,6 +168,8 @@ def tile_relativepositionmultiheadattention_pa_t_kernel(tc, q, k, x, w_v, rel_w,
             x_codes[b], x_scales[b] = x_codes_tile, x_scales_tile
 
         def value_matmul(b, n):
+            if not 0 <= b < B:
+                return
             v_bank = ps_val.tile([P, LT, KD], F32, tag="val")
             for t in range(LT):
                 nc.tensor.matmul_mx(
@@ -158,13 +184,17 @@ def tile_relativepositionmultiheadattention_pa_t_kernel(tc, q, k, x, w_v, rel_w,
             val_ps[b] = v_bank
 
         def copy_v(b, n):
+            if not 0 <= b < B:
+                return
             if n == 0:
                 v_grouped_tile = stage.tile([P, NH, KD, PACK], BF16, align_bytes=64)
                 v_grouped[b] = v_grouped_tile
-            copy_out = nc.vector.tensor_copy if n == 0 else nc.scalar.copy
+            copy_out = nc.vector.tensor_copy if n in VV else nc.scalar.copy
             copy_out(out=v_grouped[b][:, n, :, :], in_=val_ps[b][:].rearrange("p t d -> p d t"))
 
         def quantise_v(b):
+            if not 0 <= b < B:
+                return
             v_codes_tile = stage.tile([P, NH * KD], U32, align_bytes=64)
             v_scales_tile = stage.tile([P, NH * KD], U8, align_bytes=64)
             nc.vector.quantize_mx(
@@ -183,8 +213,9 @@ def tile_relativepositionmultiheadattention_pa_t_kernel(tc, q, k, x, w_v, rel_w,
                 return
             b, n = divmod(h, NH)
             pos_tile = biases.tile([P, LT, GRID_H, GRID_W], F32)
-            width = 1 if h == 0 else LT
-            for j in range(0, LT, width):
+            first = 1 if h in BIAS_HEADS else 0
+            width = 1 if h == 0 else LT - first
+            for j in range(first, LT, width):
                 nc.gpsimd.tensor_tensor(
                     out=pos_tile[:, j : j + width, :, :],
                     in0=rw_sb[b][:, LT * n + j : LT * n + j + width, :]
@@ -198,11 +229,55 @@ def tile_relativepositionmultiheadattention_pa_t_kernel(tc, q, k, x, w_v, rel_w,
                 )
             pos[h] = pos_tile
 
+        terms_sb = []
+        for s in range(2):
+            terms_tile = const.tile([P, 2, BIAS_COLS], F32, name="terms%d" % s)
+            nc.vector.memset(terms_tile[:], 0.0)
+            terms_sb.append(terms_tile)
+        spread = const.tile([P, 2, GRID_H, GRID_W], F32)
+        terms_t = {}
+
+        def make_spread():
+            for s in range(2):
+                col, row = BIAS_COLS * s, BIAS_COLS * s + GRID_W
+                nc.gpsimd.tensor_tensor(
+                    out=spread[:, s, :, :],
+                    in0=ident_f32[:, col : col + GRID_W].unsqueeze(1).to_broadcast([P, GRID_H, GRID_W]),
+                    in1=ident_f32[:, row : row + GRID_H].unsqueeze(2).to_broadcast([P, GRID_H, GRID_W]),
+                    op=ALU.add,
+                )
+
+        def bias_terms(h):
+            if h % 3 != 1 or not 0 <= h < HEADS:
+                return
+            for s in range(2):
+                b, n = divmod(h + s, NH)
+                rows = rh_sb[b][:, n, BIAS_TILE * RH_TILE_STEP : BIAS_TILE * RH_TILE_STEP + GRID_H]
+                for in_, cols in (
+                    (rw_sb[b][:, LT * n + BIAS_TILE, :], slice(0, GRID_W)),
+                    (rows, slice(GRID_W, GRID_W + GRID_H)),
+                ):
+                    nc.scalar.mul(terms_sb[h % 2][:, s, cols], in_, 1.0 / SCALE)
+
+        def transpose_terms(h):
+            if h % 3 != 1 or not 0 <= h < HEADS:
+                return
+            terms_bank = ps_qk.tile([P, P], F32, tag="qk")
+            nc.tensor.transpose(terms_bank[:], terms_sb[h % 2][:].rearrange("p s m -> p (s m)"), ident_f32[:])
+            qk_ps[h] = terms_bank
+
+        def copy_terms(h):
+            if h % 3 != 1 or not 0 <= h < HEADS:
+                return
+            terms_t_tile = heads.tile([P, P], F32)
+            nc.scalar.copy(out=terms_t_tile[:], in_=qk_ps[h][:])
+            terms_t[h] = terms_t_tile
+
         def transpose_qk(h):
             if not 0 <= h < HEADS:
                 return
             b, n = divmod(h, NH)
-            qk_bank = ps_qk.tile([P, 2, L], BF16)
+            qk_bank = ps_qk.tile([P, 2, L], BF16, tag="qk")
             for j in range(LT):
                 nc.tensor.transpose(qk_bank[:, 0, P * j : P * (j + 1)], q_sb[b][:, LT * n + j, :], ident_bf[:])
             for j in range(LT):
@@ -221,9 +296,22 @@ def tile_relativepositionmultiheadattention_pa_t_kernel(tc, q, k, x, w_v, rel_w,
                 return
             h, j = divmod(i, LT)
             sc_bank = ps_sc.tile([P, L], F32, tag="sc")
+            with_bias = h in BIAS_HEADS and j == BIAS_TILE
             nc.tensor.matmul(
-                sc_bank[:], lhsT=qk_t[h][:, 0, P * j : P * (j + 1)], rhs=qk_t[h][:, 1, :], start=True, stop=True
+                sc_bank[:],
+                lhsT=qk_t[h][:, 0, P * j : P * (j + 1)],
+                rhs=qk_t[h][:, 1, :],
+                start=True,
+                stop=not with_bias,
             )
+            if with_bias:
+                nc.tensor.matmul(
+                    sc_bank[:],
+                    lhsT=terms_t[h - (h % 3 - 1)][:],
+                    rhs=spread[:, h % 3 - 1, :, :].rearrange("p r c -> p (r c)"),
+                    start=False,
+                    stop=True,
+                )
             sc_ps[i] = sc_bank
 
         def add_bias(i):
@@ -231,6 +319,20 @@ def tile_relativepositionmultiheadattention_pa_t_kernel(tc, q, k, x, w_v, rel_w,
                 return
             h, j = divmod(i, LT)
             neg_s_tile = work.tile([P, L], F32)
+            neg_s[i] = neg_s_tile
+            neg_max_tile = stats.tile([P, 1], F32)
+            neg_max[i] = neg_max_tile
+            if h in BIAS_HEADS and j == BIAS_TILE:
+                nc.vector.tensor_scalar(
+                    out=neg_s_tile[:],
+                    in0=sc_ps[i][:],
+                    scalar1=-SCALE,
+                    scalar2=None,
+                    op0=ALU.mult,
+                    op1=ALU.min,
+                    accum_out=neg_max_tile[:],
+                )
+                return
             nc.vector.scalar_tensor_tensor(
                 out=neg_s_tile[:],
                 in0=sc_ps[i][:],
@@ -239,17 +341,15 @@ def tile_relativepositionmultiheadattention_pa_t_kernel(tc, q, k, x, w_v, rel_w,
                 op0=ALU.mult,
                 op1=ALU.subtract,
             )
-            neg_s[i] = neg_s_tile
 
         def row_minimum(i):
             if not 0 <= i < TILES:
                 return
             h, j = divmod(i, LT)
-            if j == 0:
-                neg_max_tile = stats.tile([P, LT], F32)
-                neg_max[h] = neg_max_tile
+            if h in BIAS_HEADS and j == BIAS_TILE:
+                return
             nc.vector.tensor_reduce(
-                out=neg_max[h][:, j : j + 1], in_=neg_s[i][:], axis=mybir.AxisListType.X, op=ALU.min
+                out=neg_max[i][:], in_=neg_s[i][:], axis=mybir.AxisListType.X, op=ALU.min
             )
 
         def exponent(i):
@@ -264,7 +364,7 @@ def tile_relativepositionmultiheadattention_pa_t_kernel(tc, q, k, x, w_v, rel_w,
                 out=e_tile[:],
                 in_=neg_s[i][:],
                 func=ACT.Exp,
-                bias=neg_max[h][:, j : j + 1],
+                bias=neg_max[i][:],
                 scale=-1.0,
                 accum_out=row_sum[h][:, j : j + 1],
             )
@@ -291,6 +391,8 @@ def tile_relativepositionmultiheadattention_pa_t_kernel(tc, q, k, x, w_v, rel_w,
         def quantise_e(h):
             if not 0 <= h < HEADS:
                 return
+            inv_sum_tile = stats.tile([P, LT], F32)
+            nc.vector.reciprocal(out=inv_sum_tile[:], in_=row_sum[h][:])
             e_codes_tile = heads.tile([P, L], U32, align_bytes=64)
             e_scales_tile = heads.tile([P, L], U8, align_bytes=64)
             nc.vector.quantize_mx(
@@ -298,11 +400,9 @@ def tile_relativepositionmultiheadattention_pa_t_kernel(tc, q, k, x, w_v, rel_w,
                 scales=e_scales_tile[:],
                 in_=e_grouped[h][:].rearrange("p j m t -> p (j m t)"),
             )
-            inv_sum_tile = stats.tile([P, LT], F32)
-            nc.vector.reciprocal(out=inv_sum_tile[:], in_=row_sum[h][:])
             e_codes[h], e_scales[h], inv_sum[h] = e_codes_tile, e_scales_tile, inv_sum_tile
 
-        o_ps = {}
+        o_ps, o_sb = {}, {}
 
         def output_matmul(h):
             if not 0 <= h < HEADS:
@@ -321,67 +421,81 @@ def tile_relativepositionmultiheadattention_pa_t_kernel(tc, q, k, x, w_v, rel_w,
                 )
             o_ps[h] = o_bank
 
-        def normalise(h):
+        def normalise(h, first, last):
             if not 0 <= h < HEADS:
                 return
             b, n = divmod(h, NH)
-            o_tile = heads.tile([P, LT, KD], F32)
-            for j in range(LT):
+            if first == 0:
+                o_tile = heads.tile([P, LT, KD], F32)
+                o_sb[h] = o_tile
+            for j in range(first, last):
                 nc.scalar.activation(
-                    out=o_tile[:, j, :], in_=o_ps[h][:, j, :], func=ACT.Copy, scale=inv_sum[h][:, j : j + 1]
+                    out=o_sb[h][:, j, :], in_=o_ps[h][:, j, :], func=ACT.Copy, scale=inv_sum[h][:, j : j + 1]
                 )
-            nc.sync.dma_start(
-                out=out[b].rearrange("h w c -> (h w) c").rearrange("(j p) c -> p j c", p=P)[
-                    :, :, KD * n : KD * (n + 1)
-                ],
-                in_=o_tile[:],
-            )
+            if last == LT:
+                nc.sync.dma_start(
+                    out=out[b].rearrange("h w c -> (h w) c").rearrange("(j p) c -> p j c", p=P)[
+                        :, :, KD * n : KD * (n + 1)
+                    ],
+                    in_=o_sb[h][:],
+                )
 
         with tc.manual_schedule():
             load_queries_and_keys(0, 0, 1)
             load_bias_tables(0)
-            load_w()
             load_x(0)
+            load_w()
             load_queries_and_keys(0, 1, NH)
             load_x(1)
             load_bias_tables(1)
             load_queries_and_keys(1)
             quantise_w()
-            for i in range(-12, LT * (HEADS + 2)):
+            for i in range(-16, LT * (HEADS + 3)):
                 h, j = divmod(i, LT)
-                vb, r = divmod(i + 4, LT * NH)
-                make_values = 0 <= vb < B
+                vb, r = divmod(i + 12, LT * NH)
                 if i >= 0 and i % (NH * LT) == 0:
                     load_x(h // NH + 2)
                     load_bias_tables(h // NH + 2)
                     load_queries_and_keys(h // NH + 2)
-                if j == 0:
-                    transpose_qk(h + 2)
-                scores_matmul(i + 5)
-                add_bias(i + 3)
+                scores_matmul(i + SC)
+                add_bias(i + AD)
                 if j == 0:
                     quantise_e(h - 2)
-                    if make_values and r == 4:
+                    if r == QX:
                         quantise_x(vb)
-                    if make_values and r == 12:
-                        quantise_v(vb)
+                    if r == QV:
+                        quantise_v(vb - 1)
                     position_bias(h + 3)
-                row_minimum(i + 2)
+                    bias_terms(h + 3)
+                if i == -11:
+                    make_spread()
+                row_minimum(i + MN)
+                if CEF:
+                    copy_e(i - CE)
                 exponent(i)
+                transpose_e(i - TE)
+                if not CEF:
+                    copy_e(i - CE)
                 if j == 0:
-                    output_matmul(h - 2)
-                transpose_e(i)
-                copy_e(i - 1)
-                if make_values:
-                    if r in (1, 2):
-                        copy_x(vb, r - 1)
-                    if r in (0, 1):
-                        transpose_x(vb, r)
-                    if r in (6, 7, 8, 9):
-                        copy_v(vb, r - 6)
-                    if r in (5, 6, 7, 8):
-                        value_matmul(vb, r - 5)
-                if j == 2:
+                    transpose_qk(h + 2)
+                if j == 1:
                     copy_qk(h + 2)
+                if j == 2:
+                    transpose_terms(h + 3)
                 if j == 3:
-                    normalise(h - 2)
+                    copy_terms(h + 3)
+                if j == OJ:
+                    output_matmul(h - 2)
+                for n, s in enumerate(NORM):
+                    if j == s % LT:
+                        normalise(h - 2 - s // LT, 2 * n, 2 * n + 2)
+                for a in range(2):
+                    if r == TX[a] % 16:
+                        transpose_x(vb - TX[a] // 16, a)
+                    if r == (TX[a] + 1) % 16:
+                        copy_x(vb - (TX[a] + 1) // 16, a)
+                for n in range(NH):
+                    if r == VC[n] % 16:
+                        copy_v(vb - VC[n] // 16, n)
+                    if r == VM[n] % 16:
+                        value_matmul(vb - VM[n] // 16, n)

@@ -18,6 +18,7 @@ P = 128
 PACK = 4
 LT = L // P
 HEADS = B * NH
+PAIRS = HEADS // 2
 TILES = HEADS * LT
 ROWS_PER_TILE = P // GRID_W
 SCALE = 1.0 / math.sqrt(KD)
@@ -27,24 +28,35 @@ RH_ROW_STEP = REL_H - 1
 RH_TILE_STEP = ROWS_PER_TILE * RH_ROW_STEP
 RH_RUN = (LT - 1) * RH_TILE_STEP + GRID_H
 
-BIAS_HEADS = tuple(h for h in range(HEADS) if h % 3 != 0)
+R = 1
+BIAS_HEADS = tuple(h for h in range(R, HEADS) if h % 3 != R)
 BIAS_TILE = 0
 BIAS_COLS = P // 2
 
 SC = 5
 TE = 1
 CE = 2
-TX = (1, 3)
-VM = (9, 11, 13, 15)
-VC = (10, 12, 14, 16)
-QX = 8
-QV = 4
+TX = (-11, -9)
+XC = (-10, -8)
+XV = ()
+VM = (-2, 0, 2, 9)
+VC = (-1, 1, 4, 11)
+QX = -4
+QV = 12
+OM = 1
+NM = 2
+NV = ()
+EARLY = False
+QKC = 1
+QKT = 3
+TM = 2
+VM0 = (0, 2, 3, 9)
+VC0 = (1, 3, 4, 11)
+QX0 = -1
+LQ = "nc.sync"
 AD = 3
 MN = 2
-CEF = False
-VV = (0,)
-OJ = 1
-NORM = (2, 3)
+VV = (2, 3)
 FLOPS = 2 * B * L * C * C + 2 * 2 * B * NH * L * L * KD
 
 
@@ -55,7 +67,7 @@ def tile_relativepositionmultiheadattention_pa_t_kernel(tc, q, k, x, w_v, rel_w,
         loads = ctx.enter_context(tc.tile_pool(name="loads", bufs=3))
         x_pool = ctx.enter_context(tc.tile_pool(name="x_pool", bufs=3))
         stage = ctx.enter_context(tc.tile_pool(name="stage", bufs=2))
-        biases = ctx.enter_context(tc.tile_pool(name="biases", bufs=3))
+        biases = ctx.enter_context(tc.tile_pool(name="biases", bufs=2))
         heads = ctx.enter_context(tc.tile_pool(name="heads", bufs=2))
         stats = ctx.enter_context(tc.tile_pool(name="stats", bufs=8))
         grouped = ctx.enter_context(tc.tile_pool(name="grouped", bufs=3))
@@ -73,24 +85,26 @@ def tile_relativepositionmultiheadattention_pa_t_kernel(tc, q, k, x, w_v, rel_w,
 
         q_sb, k_sb, rw_sb, rh_sb, x_sb = {}, {}, {}, {}, {}
 
-        def load_bias_tables(b):
+        def load_bias_tables(b, first_head=0, last_head=NH, queue=nc.sync):
             if not 0 <= b < B:
                 return
-            rw = loads.tile([P, NH * LT, GRID_W], BF16)
+            if first_head == 0:
+                rw = loads.tile([P, NH * LT, GRID_W], BF16)
+                rh = loads.tile([P, NH, LT * RH_TILE_STEP], BF16)
+                rw_sb[b], rh_sb[b] = rw, rh
+            tiles, some = slice(LT * first_head, LT * last_head), slice(first_head, last_head)
             rw_view = (
                 rel_w[b]
                 .rearrange("n r c m -> (n r) (c m)")[:, GRID_W - 1 : GRID_W - 1 + GRID_W * (REL_W - 1)]
                 .rearrange("a (c m) -> a c m", m=REL_W - 1)[:, :, 0:GRID_W]
                 .rearrange("(g s) c m -> s c g m", s=ROWS_PER_TILE)
             )
-            rh = loads.tile([P, NH, LT * RH_TILE_STEP], BF16)
             rh_view = rel_h[b].rearrange("n c r m -> c n (r m)")
             for s in range(ROWS_PER_TILE):
                 rows = slice(GRID_W * s, GRID_W * (s + 1))
-                nc.sync.dma_start(out=rw[rows, :, :], in_=rw_view[s])
+                queue.dma_start(out=rw_sb[b][rows, tiles, :], in_=rw_view[s][:, tiles, :])
                 first = GRID_H - 1 + RH_ROW_STEP * s
-                nc.sync.dma_start(out=rh[rows, :, 0:RH_RUN], in_=rh_view[:, :, first : first + RH_RUN])
-            rw_sb[b], rh_sb[b] = rw, rh
+                queue.dma_start(out=rh_sb[b][rows, some, 0:RH_RUN], in_=rh_view[:, some, first : first + RH_RUN])
 
         def load_queries_and_keys(b, first_head=0, last_head=NH):
             if not 0 <= b < B:
@@ -123,26 +137,29 @@ def tile_relativepositionmultiheadattention_pa_t_kernel(tc, q, k, x, w_v, rel_w,
         def load_w():
             nc.sync.dma_start(out=w_sb[:], in_=w_v.rearrange("(u p e) n -> p u e n", u=2, e=2))
 
-        def quantise_w():
-            w_grouped = const.tile([P, C, PACK], BF16, align_bytes=64)
+        w_grouped = const.tile([P, C, PACK], BF16, align_bytes=64)
+
+        def copy_w():
             nc.scalar.copy(out=w_grouped[:], in_=w_sb[:].rearrange("p u e n -> p n (u e)"))
+
+        def quantise_w():
             nc.vector.quantize_mx(
                 out=w_codes[:].bitcast(FP8X4),
                 scales=w_scales[:],
                 in_=w_grouped[:].rearrange("p n t -> p (n t)"),
             )
 
-        def transpose_x(b, a):
+        def transpose_x(b, a, pool=ps_val, tag="val"):
             if not 0 <= b < B:
                 return
             x_words = x_sb[b][:].bitcast(F32)
-            xt_bank = ps_val.tile([P, 2, 2, P], F32, tag="val")
+            xt_bank = pool.tile([P, 2, 2, P], F32, tag=tag)
             for i in range(2):
                 for u in range(2):
                     nc.tensor.transpose(
                         xt_bank[:, i, u, :], x_words[:, 2 * a + i, P * u : P * (u + 1)], ident_f32[:]
                     )
-            val_ps[b] = xt_bank
+            val_ps[b, a] = xt_bank
 
         def copy_x(b, a):
             if not 0 <= b < B:
@@ -150,9 +167,10 @@ def tile_relativepositionmultiheadattention_pa_t_kernel(tc, q, k, x, w_v, rel_w,
             if a == 0:
                 x_grouped_tile = stage.tile([P, LT, P, PACK], BF16, align_bytes=64)
                 x_grouped[b] = x_grouped_tile
-            nc.scalar.copy(
+            copy_out = nc.vector.tensor_copy if b == 0 and a in XV else nc.scalar.copy
+            copy_out(
                 out=x_grouped[b][:].bitcast(F32)[:, 2 * a : 2 * a + 2, :, :],
-                in_=val_ps[b][:].rearrange("p i u l -> p i l u"),
+                in_=val_ps[b, a][:].rearrange("p i u l -> p i l u"),
             )
 
         def quantise_x(b):
@@ -167,10 +185,10 @@ def tile_relativepositionmultiheadattention_pa_t_kernel(tc, q, k, x, w_v, rel_w,
             )
             x_codes[b], x_scales[b] = x_codes_tile, x_scales_tile
 
-        def value_matmul(b, n):
+        def value_matmul(b, n, pool=ps_val, tag="val"):
             if not 0 <= b < B:
                 return
-            v_bank = ps_val.tile([P, LT, KD], F32, tag="val")
+            v_bank = pool.tile([P, LT, KD], F32, tag=tag)
             for t in range(LT):
                 nc.tensor.matmul_mx(
                     out=v_bank[:, t, :],
@@ -181,7 +199,7 @@ def tile_relativepositionmultiheadattention_pa_t_kernel(tc, q, k, x, w_v, rel_w,
                     start=True,
                     stop=True,
                 )
-            val_ps[b] = v_bank
+            val_ps[b, n] = v_bank
 
         def copy_v(b, n):
             if not 0 <= b < B:
@@ -190,7 +208,7 @@ def tile_relativepositionmultiheadattention_pa_t_kernel(tc, q, k, x, w_v, rel_w,
                 v_grouped_tile = stage.tile([P, NH, KD, PACK], BF16, align_bytes=64)
                 v_grouped[b] = v_grouped_tile
             copy_out = nc.vector.tensor_copy if n in VV else nc.scalar.copy
-            copy_out(out=v_grouped[b][:, n, :, :], in_=val_ps[b][:].rearrange("p t d -> p d t"))
+            copy_out(out=v_grouped[b][:, n, :, :], in_=val_ps[b, n][:].rearrange("p t d -> p d t"))
 
         def quantise_v(b):
             if not 0 <= b < B:
@@ -208,26 +226,29 @@ def tile_relativepositionmultiheadattention_pa_t_kernel(tc, q, k, x, w_v, rel_w,
         e_grouped, e_codes, e_scales = {}, {}, {}
         sc_ps, neg_s, e_sb, et_ps = {}, {}, {}, {}
 
-        def position_bias(h):
-            if not 0 <= h < HEADS:
+        def position_bias(g):
+            if not 0 <= g < PAIRS:
                 return
-            b, n = divmod(h, NH)
-            pos_tile = biases.tile([P, LT, GRID_H, GRID_W], F32)
-            first = 1 if h in BIAS_HEADS else 0
-            width = 1 if h == 0 else LT - first
-            for j in range(first, LT, width):
-                nc.gpsimd.tensor_tensor(
-                    out=pos_tile[:, j : j + width, :, :],
-                    in0=rw_sb[b][:, LT * n + j : LT * n + j + width, :]
-                    .unsqueeze(2)
-                    .to_broadcast([P, width, GRID_H, GRID_W]),
-                    in1=rh_sb[b][:, n, :]
-                    .rearrange("p (j m) -> p j m", m=RH_TILE_STEP)[:, j : j + width, 0:GRID_H]
-                    .unsqueeze(3)
-                    .to_broadcast([P, width, GRID_H, GRID_W]),
-                    op=ALU.add,
-                )
-            pos[h] = pos_tile
+            pos_tile = biases.tile([P, 2, LT, GRID_H, GRID_W], F32)
+            for a in range(2):
+                h = 2 * g + a
+                b, n = divmod(h, NH)
+                first = BIAS_TILE + 1 if h in BIAS_HEADS else 0
+                width = 1 if g == 0 else LT - first
+                for j in range(first, LT, width):
+                    engine = nc.vector if (h, j) == (0, 0) else nc.gpsimd
+                    engine.tensor_tensor(
+                        out=pos_tile[:, a, j : j + width, :, :],
+                        in0=rw_sb[b][:, LT * n + j : LT * n + j + width, :]
+                        .unsqueeze(2)
+                        .to_broadcast([P, width, GRID_H, GRID_W]),
+                        in1=rh_sb[b][:, n, :]
+                        .rearrange("p (j m) -> p j m", m=RH_TILE_STEP)[:, j : j + width, 0:GRID_H]
+                        .unsqueeze(3)
+                        .to_broadcast([P, width, GRID_H, GRID_W]),
+                        op=ALU.add,
+                    )
+                pos[h] = pos_tile[:, a, :, :, :]
 
         terms_sb = []
         for s in range(2):
@@ -240,7 +261,7 @@ def tile_relativepositionmultiheadattention_pa_t_kernel(tc, q, k, x, w_v, rel_w,
         def make_spread():
             for s in range(2):
                 col, row = BIAS_COLS * s, BIAS_COLS * s + GRID_W
-                nc.gpsimd.tensor_tensor(
+                nc.vector.tensor_tensor(
                     out=spread[:, s, :, :],
                     in0=ident_f32[:, col : col + GRID_W].unsqueeze(1).to_broadcast([P, GRID_H, GRID_W]),
                     in1=ident_f32[:, row : row + GRID_H].unsqueeze(2).to_broadcast([P, GRID_H, GRID_W]),
@@ -248,7 +269,7 @@ def tile_relativepositionmultiheadattention_pa_t_kernel(tc, q, k, x, w_v, rel_w,
                 )
 
         def bias_terms(h):
-            if h % 3 != 1 or not 0 <= h < HEADS:
+            if h % 3 != (R + 1) % 3 or not R <= h < HEADS:
                 return
             for s in range(2):
                 b, n = divmod(h + s, NH)
@@ -259,18 +280,19 @@ def tile_relativepositionmultiheadattention_pa_t_kernel(tc, q, k, x, w_v, rel_w,
                 ):
                     nc.scalar.mul(terms_sb[h % 2][:, s, cols], in_, 1.0 / SCALE)
 
-        def transpose_terms(h):
-            if h % 3 != 1 or not 0 <= h < HEADS:
+        def transpose_terms(h, i):
+            if h % 3 != (R + 1) % 3 or not R <= h < HEADS:
                 return
-            terms_bank = ps_qk.tile([P, P], F32, tag="qk")
-            nc.tensor.transpose(terms_bank[:], terms_sb[h % 2][:].rearrange("p s m -> p (s m)"), ident_f32[:])
-            qk_ps[h] = terms_bank
+            if i < 0:
+                et_bank = ps_et.tile([P, 4, P], F32, tag="et")
+                et_ps[i] = et_bank
+            nc.tensor.transpose(et_ps[i][:, 2, :], terms_sb[h % 2][:].rearrange("p s m -> p (s m)"), ident_f32[:])
 
-        def copy_terms(h):
-            if h % 3 != 1 or not 0 <= h < HEADS:
+        def copy_terms(h, i):
+            if h % 3 != (R + 1) % 3 or not R <= h < HEADS:
                 return
             terms_t_tile = heads.tile([P, P], F32)
-            nc.scalar.copy(out=terms_t_tile[:], in_=qk_ps[h][:])
+            nc.scalar.copy(out=terms_t_tile[:], in_=et_ps[i][:, 2, :])
             terms_t[h] = terms_t_tile
 
         def transpose_qk(h):
@@ -307,8 +329,8 @@ def tile_relativepositionmultiheadattention_pa_t_kernel(tc, q, k, x, w_v, rel_w,
             if with_bias:
                 nc.tensor.matmul(
                     sc_bank[:],
-                    lhsT=terms_t[h - (h % 3 - 1)][:],
-                    rhs=spread[:, h % 3 - 1, :, :].rearrange("p r c -> p (r c)"),
+                    lhsT=terms_t[h - (h + 2 - R) % 3][:],
+                    rhs=spread[:, (h + 2 - R) % 3, :, :].rearrange("p r c -> p (r c)"),
                     start=False,
                     stop=True,
                 )
@@ -356,9 +378,10 @@ def tile_relativepositionmultiheadattention_pa_t_kernel(tc, q, k, x, w_v, rel_w,
             if not 0 <= i < TILES:
                 return
             h, j = divmod(i, LT)
-            if j == 0:
-                row_sum_tile = stats.tile([P, LT], F32)
-                row_sum[h] = row_sum_tile
+            g, k = divmod(i, 2 * LT)
+            if k == 0:
+                row_sum_tile = stats.tile([P, 2 * LT], F32)
+                row_sum[g] = row_sum_tile
             e_tile = work.tile([P, L], BF16)
             nc.scalar.activation(
                 out=e_tile[:],
@@ -366,7 +389,7 @@ def tile_relativepositionmultiheadattention_pa_t_kernel(tc, q, k, x, w_v, rel_w,
                 func=ACT.Exp,
                 bias=neg_max[i][:],
                 scale=-1.0,
-                accum_out=row_sum[h][:, j : j + 1],
+                accum_out=row_sum[g][:, k : k + 1],
             )
             e_sb[i] = e_tile
 
@@ -374,7 +397,7 @@ def tile_relativepositionmultiheadattention_pa_t_kernel(tc, q, k, x, w_v, rel_w,
             if not 0 <= i < TILES:
                 return
             e_words = e_sb[i][:].bitcast(F32)
-            et_bank = ps_et.tile([P, 2, P], F32, tag="et")
+            et_bank = ps_et.tile([P, 4, P], F32, tag="et")
             for u in range(2):
                 nc.tensor.transpose(et_bank[:, u, :], e_words[:, P * u : P * (u + 1)], ident_f32[:])
             et_ps[i] = et_bank
@@ -382,25 +405,27 @@ def tile_relativepositionmultiheadattention_pa_t_kernel(tc, q, k, x, w_v, rel_w,
         def copy_e(i):
             if not 0 <= i < TILES:
                 return
-            h, j = divmod(i, LT)
-            if j == 0:
-                e_grouped_tile = grouped.tile([P, LT, P, PACK], BF16, align_bytes=64)
-                e_grouped[h] = e_grouped_tile
-            nc.scalar.copy(out=e_grouped[h][:].bitcast(F32)[:, j, :, :], in_=et_ps[i][:].rearrange("p u m -> p m u"))
+            g, k = divmod(i, 2 * LT)
+            if k == 0:
+                e_grouped_tile = grouped.tile([P, 2 * LT, P, PACK], BF16, align_bytes=64)
+                e_grouped[g] = e_grouped_tile
+            nc.scalar.copy(out=e_grouped[g][:].bitcast(F32)[:, k, :, :], in_=et_ps[i][:, 0:2, :].rearrange("p u m -> p m u"))
 
-        def quantise_e(h):
-            if not 0 <= h < HEADS:
+        def quantise_e(g, first=0, last=2):
+            if not 0 <= g < PAIRS:
                 return
-            inv_sum_tile = stats.tile([P, LT], F32)
-            nc.vector.reciprocal(out=inv_sum_tile[:], in_=row_sum[h][:])
-            e_codes_tile = heads.tile([P, L], U32, align_bytes=64)
-            e_scales_tile = heads.tile([P, L], U8, align_bytes=64)
+            if first == 0:
+                inv_sum_tile = stats.tile([P, 2 * LT], F32)
+                e_codes_tile = heads.tile([P, 2 * L], U32, align_bytes=64)
+                e_scales_tile = heads.tile([P, 2 * L], U8, align_bytes=64)
+                e_codes[g], e_scales[g], inv_sum[g] = e_codes_tile, e_scales_tile, inv_sum_tile
+            tiles, cols = slice(LT * first, LT * last), slice(L * first, L * last)
+            nc.vector.reciprocal(out=inv_sum[g][:, tiles], in_=row_sum[g][:, tiles])
             nc.vector.quantize_mx(
-                out=e_codes_tile[:].bitcast(FP8X4),
-                scales=e_scales_tile[:],
-                in_=e_grouped[h][:].rearrange("p j m t -> p (j m t)"),
+                out=e_codes[g][:, cols].bitcast(FP8X4),
+                scales=e_scales[g][:, cols],
+                in_=e_grouped[g][:, tiles, :, :].rearrange("p k m t -> p (k m t)"),
             )
-            e_codes[h], e_scales[h], inv_sum[h] = e_codes_tile, e_scales_tile, inv_sum_tile
 
         o_ps, o_sb = {}, {}
 
@@ -408,12 +433,13 @@ def tile_relativepositionmultiheadattention_pa_t_kernel(tc, q, k, x, w_v, rel_w,
             if not 0 <= h < HEADS:
                 return
             b, n = divmod(h, NH)
-            o_bank = ps_o.tile([P, LT, KD], F32)
+            o_bank = ps_o.tile([P, LT, KD], F32, tag="o")
             for j in range(LT):
+                cols = slice(P * (LT * (h % 2) + j), P * (LT * (h % 2) + j + 1))
                 nc.tensor.matmul_mx(
                     out=o_bank[:, j, :],
-                    lhsT=e_codes[h][:, P * j : P * (j + 1)].bitcast(FP8X4),
-                    lhsT_scale=e_scales[h][:, P * j : P * (j + 1)],
+                    lhsT=e_codes[h // 2][:, cols].bitcast(FP8X4),
+                    lhsT_scale=e_scales[h // 2][:, cols],
                     rhs=v_codes[b][:, KD * n : KD * (n + 1)].bitcast(FP8X4),
                     rhs_scale=v_scales[b][:, KD * n : KD * (n + 1)],
                     start=True,
@@ -421,16 +447,26 @@ def tile_relativepositionmultiheadattention_pa_t_kernel(tc, q, k, x, w_v, rel_w,
                 )
             o_ps[h] = o_bank
 
-        def normalise(h, first, last):
+        def normalise(h, first, last, on_vector=False):
             if not 0 <= h < HEADS:
                 return
             b, n = divmod(h, NH)
             if first == 0:
                 o_tile = heads.tile([P, LT, KD], F32)
                 o_sb[h] = o_tile
-            for j in range(first, last):
+            if not 0 <= h < HEADS:
+                return
+            factors = inv_sum[h // 2][:, LT * (h % 2) : LT * (h % 2 + 1)]
+            if on_vector:
+                nc.vector.tensor_tensor(
+                    out=o_sb[h][:, first:last, :],
+                    in0=o_ps[h][:, first:last, :],
+                    in1=factors[:, first:last].unsqueeze(2).to_broadcast([P, last - first, KD]),
+                    op=ALU.mult,
+                )
+            for j in () if on_vector else range(first, last):
                 nc.scalar.activation(
-                    out=o_sb[h][:, j, :], in_=o_ps[h][:, j, :], func=ACT.Copy, scale=inv_sum[h][:, j : j + 1]
+                    out=o_sb[h][:, j, :], in_=o_ps[h][:, j, :], func=ACT.Copy, scale=factors[:, j : j + 1]
                 )
             if last == LT:
                 nc.sync.dma_start(
@@ -440,62 +476,117 @@ def tile_relativepositionmultiheadattention_pa_t_kernel(tc, q, k, x, w_v, rel_w,
                     in_=o_sb[h][:],
                 )
 
+        tensor_steps, copy_steps, quantise_steps = {}, {}, {}
+        for b in range(B):
+            base = LT * NH * b
+            quantise_steps.setdefault(base + QV, []).append((quantise_v, b))
+            if b > 0:
+                quantise_steps.setdefault(base + QX, []).append((quantise_x, b))
+                for a in range(2):
+                    copy_steps.setdefault(base + XC[a], []).append((copy_x, b, a))
+                    tensor_steps.setdefault(base + TX[a], []).append((transpose_x, b, a))
+            for n in range(NH):
+                copy_steps.setdefault((VC if b else VC0)[n] + base, []).append((copy_v, b, n))
+                tensor_steps.setdefault((VM if b else VM0)[n] + base, []).append((value_matmul, b, n))
+
         with tc.manual_schedule():
             load_queries_and_keys(0, 0, 1)
-            load_bias_tables(0)
-            load_x(0)
+            load_bias_tables(0, 0, 1, nc.scalar)
             load_w()
-            load_queries_and_keys(0, 1, NH)
+            load_x(0)
+            load_queries_and_keys(0, 1, 2)
+            load_bias_tables(0, 1, NH)
+            load_queries_and_keys(0, 2, NH)
             load_x(1)
             load_bias_tables(1)
             load_queries_and_keys(1)
+            make_spread()
+            position_bias(0)
+            transpose_qk(0)
+            copy_qk(0)
+            for i in range(3):
+                scores_matmul(i)
+            add_bias(0)
+            row_minimum(0)
+            copy_w()
+            exponent(0)
+            transpose_x(0, 0)
+            transpose_x(0, 1, ps_o, "o")
+            copy_x(0, 0)
+            copy_x(0, 1)
+            add_bias(1)
+            row_minimum(1)
             quantise_w()
-            for i in range(-16, LT * (HEADS + 3)):
+            for i in range(-8, TILES + 2):
                 h, j = divmod(i, LT)
-                vb, r = divmod(i + 12, LT * NH)
+                g, step = divmod(i - 4, 2 * LT)
                 if i >= 0 and i % (NH * LT) == 0:
                     load_x(h // NH + 2)
                     load_bias_tables(h // NH + 2)
                     load_queries_and_keys(h // NH + 2)
-                scores_matmul(i + SC)
-                add_bias(i + AD)
+                if i + SC >= 3:
+                    scores_matmul(i + SC)
+                for stage_of, b, part in tensor_steps.get(i, ()):
+                    if EARLY and part in VV and stage_of is value_matmul:
+                        stage_of(b, part)
+                if i + AD > 1:
+                    add_bias(i + AD)
+                if i == QX0:
+                    quantise_x(0)
+                if step == 0:
+                    if g < PAIRS:
+                        quantise_e(g - 1)
+                    for stage_of, b in quantise_steps.get(i, ()):
+                        stage_of(b)
+                    if g + 2 > 0:
+                        position_bias(g + 2)
+                    if (2 * g - 3) % NH in NV and 2 * g - 3 < HEADS - 4:
+                        normalise(2 * g - 3, 0, LT, True)
                 if j == 0:
-                    quantise_e(h - 2)
-                    if r == QX:
-                        quantise_x(vb)
-                    if r == QV:
-                        quantise_v(vb - 1)
-                    position_bias(h + 3)
                     bias_terms(h + 3)
-                if i == -11:
-                    make_spread()
-                row_minimum(i + MN)
-                if CEF:
-                    copy_e(i - CE)
-                exponent(i)
+                if i + MN > 1:
+                    row_minimum(i + MN)
+                for stage_of, b, part in copy_steps.get(i, ()):
+                    if part in VV and stage_of is copy_v:
+                        stage_of(b, part)
+                if i > 0:
+                    exponent(i)
                 transpose_e(i - TE)
-                if not CEF:
-                    copy_e(i - CE)
-                if j == 0:
-                    transpose_qk(h + 2)
-                if j == 1:
+                copy_e(i - CE)
+                if j == QKC and h > -2:
                     copy_qk(h + 2)
-                if j == 2:
-                    transpose_terms(h + 3)
-                if j == 3:
-                    copy_terms(h + 3)
-                if j == OJ:
-                    output_matmul(h - 2)
-                for n, s in enumerate(NORM):
-                    if j == s % LT:
-                        normalise(h - 2 - s // LT, 2 * n, 2 * n + 2)
+                if j == TM + 1:
+                    copy_terms(h + 3, i - 2)
                 for a in range(2):
-                    if r == TX[a] % 16:
-                        transpose_x(vb - TX[a] // 16, a)
-                    if r == (TX[a] + 1) % 16:
-                        copy_x(vb - (TX[a] + 1) // 16, a)
-                for n in range(NH):
-                    if r == VC[n] % 16:
-                        copy_v(vb - VC[n] // 16, n)
-                    if r == VM[n] % 16:
-                        value_matmul(vb - VM[n] // 16, n)
+                    if g < PAIRS - 1 and (2 * (g - 1) + a) % NH not in NV:
+                        if step == NM + LT * a:
+                            normalise(2 * (g - 1) + a, 0, LT // 2)
+                        if step == NM + 1 + LT * a:
+                            normalise(2 * (g - 1) + a, LT // 2, LT)
+                if i == TILES - 3:
+                    output_matmul(HEADS - 4)
+                    normalise(HEADS - 4, 0, LT, True)
+                if i == TILES - 2:
+                    output_matmul(HEADS - 3)
+                    normalise(HEADS - 3, 0, LT, True)
+                if i == TILES - 1:
+                    quantise_e(PAIRS - 1, 0, 1)
+                    output_matmul(HEADS - 2)
+                if i == TILES + 1:
+                    normalise(HEADS - 2, 0, LT)
+                    quantise_e(PAIRS - 1, 1, 2)
+                    output_matmul(HEADS - 1)
+                    normalise(HEADS - 1, 0, LT, True)
+                for stage_of, b, part in copy_steps.get(i, ()):
+                    if part not in VV or stage_of is copy_x:
+                        stage_of(b, part)
+                if j == QKT and h + (QKT == 3) > -2:
+                    transpose_qk(h + 2 + (QKT == 3))
+                if j == TM:
+                    transpose_terms(h + 3, i - 1)
+                for a in range(2):
+                    if step == OM + LT * a and g < PAIRS - 1:
+                        output_matmul(2 * (g - 1) + a)
+                for stage_of, b, part in tensor_steps.get(i, ()):
+                    if not EARLY or part not in VV or stage_of is transpose_x:
+                        stage_of(b, part)

@@ -28,9 +28,12 @@ RH_ROW_STEP = REL_H - 1
 RH_TILE_STEP = ROWS_PER_TILE * RH_ROW_STEP
 RH_RUN = (LT - 1) * RH_TILE_STEP + GRID_H
 
-R = 1
-BIAS_HEADS = tuple(h for h in range(R, HEADS) if h % 3 != R)
+BIAS_HEADS = tuple(h for h in range(2, HEADS) if h % 2 == 0 or h % 6 == 3)
 BIAS_TILE = 0
+STARTS = (1, 2, 4)
+VPOS = (0, 1)
+TABLE_HEADS = BIAS_HEADS[::2]
+TABLE_OF = {h: BIAS_HEADS[i - i % 2] for i, h in enumerate(BIAS_HEADS)}
 BIAS_COLS = P // 2
 
 SC = 5
@@ -82,6 +85,10 @@ def tile_relativepositionmultiheadattention_pa_t_kernel(tc, q, k, x, w_v, rel_w,
         make_identity(nc, ident_bf[:])
         ident_f32 = const.tile([P, P], F32)
         make_identity(nc, ident_f32[:])
+
+        table_warm = const.tile([P, 1], F32)
+        nc.vector.memset(table_warm[:], 0.0)
+        nc.scalar.activation(out=table_warm[:], in_=table_warm[:], func=ACT.Exp)
 
         q_sb, k_sb, rw_sb, rh_sb, x_sb = {}, {}, {}, {}, {}
 
@@ -230,25 +237,31 @@ def tile_relativepositionmultiheadattention_pa_t_kernel(tc, q, k, x, w_v, rel_w,
             if not 0 <= g < PAIRS:
                 return
             pos_tile = biases.tile([P, 2, LT, GRID_H, GRID_W], F32)
+            b, n = divmod(2 * g, NH)
+            wanted = [k for k in range(2 * LT) if not (2 * g + k // LT in BIAS_HEADS and k % LT == BIAS_TILE)]
+            runs = []
+            for k in wanted:
+                if runs and runs[-1][-1] == k - 1 and (g > 0 or k not in STARTS):
+                    runs[-1].append(k)
+                else:
+                    runs.append([k])
+            tiles = pos_tile[:].rearrange("p a j r c -> p (a j) r c")
+            rows = rh_sb[b][:].rearrange("p n (j m) -> p (n j) m", m=RH_TILE_STEP)
+            for run in runs:
+                width = len(run)
+                engine = nc.vector if g == 0 and run[0] in VPOS else nc.gpsimd
+                engine.tensor_tensor(
+                    out=tiles[:, run[0] : run[0] + width, :, :],
+                    in0=rw_sb[b][:, LT * n + run[0] : LT * n + run[0] + width, :]
+                    .unsqueeze(2)
+                    .to_broadcast([P, width, GRID_H, GRID_W]),
+                    in1=rows[:, LT * n + run[0] : LT * n + run[0] + width, 0:GRID_H]
+                    .unsqueeze(3)
+                    .to_broadcast([P, width, GRID_H, GRID_W]),
+                    op=ALU.add,
+                )
             for a in range(2):
-                h = 2 * g + a
-                b, n = divmod(h, NH)
-                first = BIAS_TILE + 1 if h in BIAS_HEADS else 0
-                width = 1 if g == 0 else LT - first
-                for j in range(first, LT, width):
-                    engine = nc.vector if (h, j) == (0, 0) else nc.gpsimd
-                    engine.tensor_tensor(
-                        out=pos_tile[:, a, j : j + width, :, :],
-                        in0=rw_sb[b][:, LT * n + j : LT * n + j + width, :]
-                        .unsqueeze(2)
-                        .to_broadcast([P, width, GRID_H, GRID_W]),
-                        in1=rh_sb[b][:, n, :]
-                        .rearrange("p (j m) -> p j m", m=RH_TILE_STEP)[:, j : j + width, 0:GRID_H]
-                        .unsqueeze(3)
-                        .to_broadcast([P, width, GRID_H, GRID_W]),
-                        op=ALU.add,
-                    )
-                pos[h] = pos_tile[:, a, :, :, :]
+                pos[2 * g + a] = pos_tile[:, a, :, :, :]
 
         terms_sb = []
         for s in range(2):
@@ -269,27 +282,28 @@ def tile_relativepositionmultiheadattention_pa_t_kernel(tc, q, k, x, w_v, rel_w,
                 )
 
         def bias_terms(h):
-            if h % 3 != (R + 1) % 3 or not R <= h < HEADS:
+            if h not in TABLE_HEADS:
                 return
-            for s in range(2):
-                b, n = divmod(h + s, NH)
+            k = BIAS_HEADS.index(h)
+            for s, head in enumerate(BIAS_HEADS[k : k + 2]):
+                b, n = divmod(head, NH)
                 rows = rh_sb[b][:, n, BIAS_TILE * RH_TILE_STEP : BIAS_TILE * RH_TILE_STEP + GRID_H]
                 for in_, cols in (
                     (rw_sb[b][:, LT * n + BIAS_TILE, :], slice(0, GRID_W)),
                     (rows, slice(GRID_W, GRID_W + GRID_H)),
                 ):
-                    nc.scalar.mul(terms_sb[h % 2][:, s, cols], in_, 1.0 / SCALE)
+                    nc.scalar.mul(terms_sb[TABLE_HEADS.index(h) % 2][:, s, cols], in_, 1.0 / SCALE)
 
         def transpose_terms(h, i):
-            if h % 3 != (R + 1) % 3 or not R <= h < HEADS:
+            if h not in TABLE_HEADS:
                 return
             if i < 0:
                 et_bank = ps_et.tile([P, 4, P], F32, tag="et")
                 et_ps[i] = et_bank
-            nc.tensor.transpose(et_ps[i][:, 2, :], terms_sb[h % 2][:].rearrange("p s m -> p (s m)"), ident_f32[:])
+            nc.tensor.transpose(et_ps[i][:, 2, :], terms_sb[TABLE_HEADS.index(h) % 2][:].rearrange("p s m -> p (s m)"), ident_f32[:])
 
         def copy_terms(h, i):
-            if h % 3 != (R + 1) % 3 or not R <= h < HEADS:
+            if h not in TABLE_HEADS:
                 return
             terms_t_tile = heads.tile([P, P], F32)
             nc.scalar.copy(out=terms_t_tile[:], in_=et_ps[i][:, 2, :])
@@ -329,8 +343,8 @@ def tile_relativepositionmultiheadattention_pa_t_kernel(tc, q, k, x, w_v, rel_w,
             if with_bias:
                 nc.tensor.matmul(
                     sc_bank[:],
-                    lhsT=terms_t[h - (h + 2 - R) % 3][:],
-                    rhs=spread[:, (h + 2 - R) % 3, :, :].rearrange("p r c -> p (r c)"),
+                    lhsT=terms_t[TABLE_OF[h]][:],
+                    rhs=spread[:, BIAS_HEADS.index(h) % 2, :, :].rearrange("p r c -> p (r c)"),
                     start=False,
                     stop=True,
                 )
@@ -491,11 +505,11 @@ def tile_relativepositionmultiheadattention_pa_t_kernel(tc, q, k, x, w_v, rel_w,
 
         with tc.manual_schedule():
             load_queries_and_keys(0, 0, 1)
-            load_bias_tables(0, 0, 1, nc.scalar)
+            load_bias_tables(0, 0, 2)
             load_w()
             load_x(0)
             load_queries_and_keys(0, 1, 2)
-            load_bias_tables(0, 1, NH)
+            load_bias_tables(0, 2, NH)
             load_queries_and_keys(0, 2, NH)
             load_x(1)
             load_bias_tables(1)
@@ -509,14 +523,15 @@ def tile_relativepositionmultiheadattention_pa_t_kernel(tc, q, k, x, w_v, rel_w,
             add_bias(0)
             row_minimum(0)
             copy_w()
-            exponent(0)
             transpose_x(0, 0)
             transpose_x(0, 1, ps_o, "o")
             copy_x(0, 0)
             copy_x(0, 1)
+            exponent(0)
             add_bias(1)
             row_minimum(1)
             quantise_w()
+            quantise_x(0)
             for i in range(-8, TILES + 2):
                 h, j = divmod(i, LT)
                 g, step = divmod(i - 4, 2 * LT)
@@ -531,8 +546,6 @@ def tile_relativepositionmultiheadattention_pa_t_kernel(tc, q, k, x, w_v, rel_w,
                         stage_of(b, part)
                 if i + AD > 1:
                     add_bias(i + AD)
-                if i == QX0:
-                    quantise_x(0)
                 if step == 0:
                     if g < PAIRS:
                         quantise_e(g - 1)

@@ -28,7 +28,8 @@ RH_ROW_STEP = REL_H - 1
 RH_TILE_STEP = ROWS_PER_TILE * RH_ROW_STEP
 RH_RUN = (LT - 1) * RH_TILE_STEP + GRID_H
 
-BIAS_HEADS = tuple(h for h in range(2, HEADS) if h % 2 == 0 or h % 6 == 3)
+ODD = 1
+BIAS_HEADS = tuple(h for h in range(1, HEADS) if h % 2 == 0 or h % 6 == ODD)
 BIAS_TILE = 0
 STARTS = (1, 2, 4)
 VPOS = (0, 1)
@@ -72,6 +73,7 @@ def tile_relativepositionmultiheadattention_pa_t_kernel(tc, q, k, x, w_v, rel_w,
         stage = ctx.enter_context(tc.tile_pool(name="stage", bufs=2))
         biases = ctx.enter_context(tc.tile_pool(name="biases", bufs=2))
         heads = ctx.enter_context(tc.tile_pool(name="heads", bufs=2))
+        outs = ctx.enter_context(tc.tile_pool(name="outs", bufs=4))
         stats = ctx.enter_context(tc.tile_pool(name="stats", bufs=8))
         grouped = ctx.enter_context(tc.tile_pool(name="grouped", bufs=3))
         work = ctx.enter_context(tc.tile_pool(name="work", bufs=6))
@@ -285,14 +287,22 @@ def tile_relativepositionmultiheadattention_pa_t_kernel(tc, q, k, x, w_v, rel_w,
             if h not in TABLE_HEADS:
                 return
             k = BIAS_HEADS.index(h)
-            for s, head in enumerate(BIAS_HEADS[k : k + 2]):
-                b, n = divmod(head, NH)
-                rows = rh_sb[b][:, n, BIAS_TILE * RH_TILE_STEP : BIAS_TILE * RH_TILE_STEP + GRID_H]
+            pair = BIAS_HEADS[k : k + 2]
+            same_image = pair[0] // NH == pair[1] // NH
+            for s in (0,) if same_image else (0, 1):
+                b, n = divmod(pair[s], NH)
+                step = pair[1] - pair[0]
+                members = slice(n, n + step + 1, step) if same_image else slice(n, n + 1)
+                slots = slice(0, 2) if same_image else slice(s, s + 1)
+                rw_rows = rw_sb[b][:].rearrange("p (n j) c -> p n j c", j=LT)
                 for in_, cols in (
-                    (rw_sb[b][:, LT * n + BIAS_TILE, :], slice(0, GRID_W)),
-                    (rows, slice(GRID_W, GRID_W + GRID_H)),
+                    (rw_rows[:, members, BIAS_TILE, :], slice(0, GRID_W)),
+                    (
+                        rh_sb[b][:, members, BIAS_TILE * RH_TILE_STEP : BIAS_TILE * RH_TILE_STEP + GRID_H],
+                        slice(GRID_W, GRID_W + GRID_H),
+                    ),
                 ):
-                    nc.scalar.mul(terms_sb[TABLE_HEADS.index(h) % 2][:, s, cols], in_, 1.0 / SCALE)
+                    nc.scalar.mul(terms_sb[TABLE_HEADS.index(h) % 2][:, slots, cols], in_, 1.0 / SCALE)
 
         def transpose_terms(h, i):
             if h not in TABLE_HEADS:
@@ -443,11 +453,11 @@ def tile_relativepositionmultiheadattention_pa_t_kernel(tc, q, k, x, w_v, rel_w,
 
         o_ps, o_sb = {}, {}
 
-        def output_matmul(h):
+        def output_matmul(h, pool=ps_o, tag="o"):
             if not 0 <= h < HEADS:
                 return
             b, n = divmod(h, NH)
-            o_bank = ps_o.tile([P, LT, KD], F32, tag="o")
+            o_bank = pool.tile([P, LT, KD], F32, tag=tag)
             for j in range(LT):
                 cols = slice(P * (LT * (h % 2) + j), P * (LT * (h % 2) + j + 1))
                 nc.tensor.matmul_mx(
@@ -461,12 +471,12 @@ def tile_relativepositionmultiheadattention_pa_t_kernel(tc, q, k, x, w_v, rel_w,
                 )
             o_ps[h] = o_bank
 
-        def normalise(h, first, last, on_vector=False):
+        def normalise(h, first, last, on_vector=False, queue=nc.sync):
             if not 0 <= h < HEADS:
                 return
             b, n = divmod(h, NH)
             if first == 0:
-                o_tile = heads.tile([P, LT, KD], F32)
+                o_tile = outs.tile([P, LT, KD], F32)
                 o_sb[h] = o_tile
             if not 0 <= h < HEADS:
                 return
@@ -483,7 +493,7 @@ def tile_relativepositionmultiheadattention_pa_t_kernel(tc, q, k, x, w_v, rel_w,
                     out=o_sb[h][:, j, :], in_=o_ps[h][:, j, :], func=ACT.Copy, scale=factors[:, j : j + 1]
                 )
             if last == LT:
-                nc.sync.dma_start(
+                queue.dma_start(
                     out=out[b].rearrange("h w c -> (h w) c").rearrange("(j p) c -> p j c", p=P)[
                         :, :, KD * n : KD * (n + 1)
                     ],
@@ -528,27 +538,28 @@ def tile_relativepositionmultiheadattention_pa_t_kernel(tc, q, k, x, w_v, rel_w,
             copy_x(0, 0)
             copy_x(0, 1)
             exponent(0)
-            add_bias(1)
-            row_minimum(1)
+            scores_matmul(3)
+            for i in range(1, 4):
+                add_bias(i)
+                row_minimum(i)
             quantise_w()
             quantise_x(0)
-            for i in range(-8, TILES + 2):
+            for i in range(-8, TILES):
                 h, j = divmod(i, LT)
                 g, step = divmod(i - 4, 2 * LT)
                 if i >= 0 and i % (NH * LT) == 0:
                     load_x(h // NH + 2)
                     load_bias_tables(h // NH + 2)
                     load_queries_and_keys(h // NH + 2)
-                if i + SC >= 3:
+                if i + SC > 3:
                     scores_matmul(i + SC)
                 for stage_of, b, part in tensor_steps.get(i, ()):
                     if EARLY and part in VV and stage_of is value_matmul:
                         stage_of(b, part)
-                if i + AD > 1:
+                if i + AD > 3:
                     add_bias(i + AD)
-                if step == 0:
-                    if g < PAIRS:
-                        quantise_e(g - 1)
+                if step == 0 and i < TILES - LT:
+                    quantise_e(g - 1)
                     for stage_of, b in quantise_steps.get(i, ()):
                         stage_of(b)
                     if g + 2 > 0:
@@ -557,7 +568,7 @@ def tile_relativepositionmultiheadattention_pa_t_kernel(tc, q, k, x, w_v, rel_w,
                         normalise(2 * g - 3, 0, LT, True)
                 if j == 0:
                     bias_terms(h + 3)
-                if i + MN > 1:
+                if i + MN > 3:
                     row_minimum(i + MN)
                 for stage_of, b, part in copy_steps.get(i, ()):
                     if part in VV and stage_of is copy_v:
@@ -576,20 +587,6 @@ def tile_relativepositionmultiheadattention_pa_t_kernel(tc, q, k, x, w_v, rel_w,
                             normalise(2 * (g - 1) + a, 0, LT // 2)
                         if step == NM + 1 + LT * a:
                             normalise(2 * (g - 1) + a, LT // 2, LT)
-                if i == TILES - 3:
-                    output_matmul(HEADS - 4)
-                    normalise(HEADS - 4, 0, LT, True)
-                if i == TILES - 2:
-                    output_matmul(HEADS - 3)
-                    normalise(HEADS - 3, 0, LT, True)
-                if i == TILES - 1:
-                    quantise_e(PAIRS - 1, 0, 1)
-                    output_matmul(HEADS - 2)
-                if i == TILES + 1:
-                    normalise(HEADS - 2, 0, LT)
-                    quantise_e(PAIRS - 1, 1, 2)
-                    output_matmul(HEADS - 1)
-                    normalise(HEADS - 1, 0, LT, True)
                 for stage_of, b, part in copy_steps.get(i, ()):
                     if part not in VV or stage_of is copy_x:
                         stage_of(b, part)
@@ -603,3 +600,17 @@ def tile_relativepositionmultiheadattention_pa_t_kernel(tc, q, k, x, w_v, rel_w,
                 for stage_of, b, part in tensor_steps.get(i, ()):
                     if not EARLY or part not in VV or stage_of is transpose_x:
                         stage_of(b, part)
+            transpose_e(TILES - 1)
+            copy_e(TILES - 2)
+            copy_e(TILES - 1)
+            quantise_e(PAIRS - 2)
+            quantise_v(B - 1)
+            quantise_e(PAIRS - 1, 0, 1)
+            for a in range(3):
+                output_matmul(HEADS - 4 + a, ps_sc, "sc")
+            quantise_e(PAIRS - 1, 1, 2)
+            output_matmul(HEADS - 1)
+            normalise(HEADS - 4, 0, LT, True)
+            normalise(HEADS - 3, 0, LT, False, nc.scalar)
+            normalise(HEADS - 2, 0, LT, False, nc.scalar)
+            normalise(HEADS - 1, 0, LT, True)

@@ -40,11 +40,13 @@ BIAS_COLS = P // 2
 SC = 5
 TE = 1
 CE = 2
-TX = (-11, -9)
-XC = (-10, -8)
+TX = (-17, -13)
+XC = (-16, -12)
+TX1 = (-13, -9)
+XC1 = (-12, -8)
 XV = ()
-VM = (-2, 0, 2, 9)
-VC = (-1, 1, 4, 11)
+VM = (-3, 1, 5, 9)
+VC = (-2, 2, 7, 11)
 QX = -4
 QV = 12
 OM = 1
@@ -54,8 +56,8 @@ EARLY = False
 QKC = 1
 QKT = 3
 TM = 2
-VM0 = (0, 2, 3, 9)
-VC0 = (1, 3, 4, 11)
+VM0 = (0, 1, 5, 9)
+VC0 = (1, 2, 7, 11)
 QX0 = -1
 LQ = "nc.sync"
 AD = 3
@@ -507,8 +509,8 @@ def tile_relativepositionmultiheadattention_pa_t_kernel(tc, q, k, x, w_v, rel_w,
             if b > 0:
                 quantise_steps.setdefault(base + QX, []).append((quantise_x, b))
                 for a in range(2):
-                    copy_steps.setdefault(base + XC[a], []).append((copy_x, b, a))
-                    tensor_steps.setdefault(base + TX[a], []).append((transpose_x, b, a))
+                    copy_steps.setdefault(base + (XC1 if b == 1 else XC)[a], []).append((copy_x, b, a))
+                    tensor_steps.setdefault(base + (TX1 if b == 1 else TX)[a], []).append((transpose_x, b, a))
             for n in range(NH):
                 copy_steps.setdefault((VC if b else VC0)[n] + base, []).append((copy_v, b, n))
                 tensor_steps.setdefault((VM if b else VM0)[n] + base, []).append((value_matmul, b, n))

from contextlib import ExitStack
import math

import concourse.mybir as mybir
from concourse.masks import make_identity

F32 = mybir.dt.float32
BF16 = mybir.dt.bfloat16
U32 = mybir.dt.uint32
U8 = mybir.dt.uint8
FP8X4 = mybir.dt.float8_e4m3fn_x4
ALU = mybir.AluOpType
ACT = mybir.ActivationFunctionType

B, GRID_H, GRID_W, C, NH, KD = 10, 16, 32, 512, 4, 128
L = GRID_H * GRID_W
P = 128
PACK = 4
LT = L // P
HEADS = B * NH
PAIRS = HEADS // 2
TILES = HEADS * LT
ROWS_PER_TILE = P // GRID_W
SCALE = 1.0 / math.sqrt(KD)
REL_W = 2 * GRID_W - 1
REL_H = 2 * GRID_H - 1
RH_ROW_STEP = REL_H - 1
RH_TILE_STEP = ROWS_PER_TILE * RH_ROW_STEP
RH_RUN = (LT - 1) * RH_TILE_STEP + GRID_H

ODD = 1
BIAS_HEADS = tuple(h for h in range(1, HEADS) if h % 2 == 0 or h % 6 == ODD)
BIAS_TILE = 0
STARTS = (1, 2, 4)
VPOS = (0, 1)
TABLE_HEADS = BIAS_HEADS[::2]
TABLE_OF = {h: BIAS_HEADS[i - i % 2] for i, h in enumerate(BIAS_HEADS)}
BIAS_COLS = P // 2

SC = 5
TE = 1
CE = 2
TX = (-17, -13)
XC = (-16, -12)
TX1 = (-13, -9)
XC1 = (-12, -8)
XV = ()
VM = (-3, 1, 5, 9)
VC = (-2, 2, 7, 11)
QX = -4
QV = 12
OM = 1
NM = 2
NV = ()
EARLY = False
QKC = 1
QKT = 3
TM = 2
VM0 = (0, 1, 5, 9)
VC0 = (1, 2, 7, 11)
QX0 = -1
LQ = "nc.sync"
AD = 3
MN = 2
VV = (2, 3)
FLOPS = 2 * B * L * C * C + 2 * 2 * B * NH * L * L * KD


def tile_relativepositionmultiheadattention_pa_t_kernel(tc, q, k, x, w_v, rel_w, rel_h, out):
    nc = tc.nc
    with ExitStack() as ctx:
        const = ctx.enter_context(tc.tile_pool(name="const", bufs=1))
        loads = ctx.enter_context(tc.tile_pool(name="loads", bufs=3))
        x_pool = ctx.enter_context(tc.tile_pool(name="x_pool", bufs=3))
        stage = ctx.enter_context(tc.tile_pool(name="stage", bufs=2))
        biases = ctx.enter_context(tc.tile_pool(name="biases", bufs=2))
        heads = ctx.enter_context(tc.tile_pool(name="heads", bufs=2))
        outs = ctx.enter_context(tc.tile_pool(name="outs", bufs=4))
        stats = ctx.enter_context(tc.tile_pool(name="stats", bufs=8))
        grouped = ctx.enter_context(tc.tile_pool(name="grouped", bufs=3))
        work = ctx.enter_context(tc.tile_pool(name="work", bufs=6))
        ps_sc = ctx.enter_context(tc.psum_pool(name="ps_sc", bufs=3))
        ps_et = ctx.enter_context(tc.psum_pool(name="ps_et", bufs=2))
        ps_val = ctx.enter_context(tc.psum_pool(name="ps_val", bufs=1))
        ps_o = ctx.enter_context(tc.psum_pool(name="ps_o", bufs=1))
        ps_qk = ctx.enter_context(tc.psum_pool(name="ps_qk", bufs=1))

        ident_bf = const.tile([P, P], BF16)
        make_identity(nc, ident_bf[:])
        ident_f32 = const.tile([P, P], F32)
        make_identity(nc, ident_f32[:])

        table_warm = const.tile([P, 1], F32)
        nc.vector.memset(table_warm[:], 0.0)
        nc.scalar.activation(out=table_warm[:], in_=table_warm[:], func=ACT.Exp)

        q_sb, k_sb, rw_sb, rh_sb, x_sb = {}, {}, {}, {}, {}

        def load_bias_tables(b, first_head=0, last_head=NH, queue=nc.sync):
            if not 0 <= b < B:
                return
            if first_head == 0:
                rw = loads.tile([P, NH * LT, GRID_W], BF16)
                rh = loads.tile([P, NH, LT * RH_TILE_STEP], BF16)
                rw_sb[b], rh_sb[b] = rw, rh
            tiles, some = slice(LT * first_head, LT * last_head), slice(first_head, last_head)
            rw_view = (
                rel_w[b]
                .rearrange("n r c m -> (n r) (c m)")[:, GRID_W - 1 : GRID_W - 1 + GRID_W * (REL_W - 1)]
                .rearrange("a (c m) -> a c m", m=REL_W - 1)[:, :, 0:GRID_W]
                .rearrange("(g s) c m -> s c g m", s=ROWS_PER_TILE)
            )
            rh_view = rel_h[b].rearrange("n c r m -> c n (r m)")
            for s in range(ROWS_PER_TILE):
                rows = slice(GRID_W * s, GRID_W * (s + 1))
                queue.dma_start(out=rw_sb[b][rows, tiles, :], in_=rw_view[s][:, tiles, :])
                first = GRID_H - 1 + RH_ROW_STEP * s
                queue.dma_start(out=rh_sb[b][rows, some, 0:RH_RUN], in_=rh_view[:, some, first : first + RH_RUN])

        def load_queries_and_keys(b, first_head=0, last_head=NH):
            if not 0 <= b < B:
                return
            if first_head == 0:
                q_tile = loads.tile([P, NH * LT, KD], BF16)
                k_tile = loads.tile([P, NH * LT, KD], BF16)
                q_sb[b], k_sb[b] = q_tile, k_tile
            tiles = slice(LT * first_head, LT * last_head)
            q_view = q[b].rearrange("n (j p) d -> p (n j) d", p=P)
            k_view = k[b].rearrange("n (j p) d -> p (n j) d", p=P)
            nc.sync.dma_start(out=q_sb[b][:, tiles, :], in_=q_view[:, tiles, :])
            nc.sync.dma_start(out=k_sb[b][:, tiles, :], in_=k_view[:, tiles, :])

        def load_x(b):
            if not 0 <= b < B:
                return
            x_tile = x_pool.tile([P, LT, C], BF16)
            nc.sync.dma_start(
                out=x_tile[:].rearrange("p (u e) c -> p u e c", e=2),
                in_=x[b].rearrange("h w c -> (h w) c").rearrange("(u p e) c -> p u e c", p=P, e=2),
            )
            x_sb[b] = x_tile

        w_codes = const.tile([P, C], U32, align_bytes=64)
        w_scales = const.tile([P, C], U8, align_bytes=64)
        w_sb = const.tile([P, 2, 2, C], BF16)
        val_ps, x_grouped, x_codes, x_scales, v_grouped, v_codes, v_scales = {}, {}, {}, {}, {}, {}, {}

        def load_w():
            nc.sync.dma_start(out=w_sb[:], in_=w_v.rearrange("(u p e) n -> p u e n", u=2, e=2))

        w_grouped = const.tile([P, C, PACK], BF16, align_bytes=64)

        def copy_w():
            nc.scalar.copy(out=w_grouped[:], in_=w_sb[:].rearrange("p u e n -> p n (u e)"))

        def quantise_w():
            nc.vector.quantize_mx(
                out=w_codes[:].bitcast(FP8X4),
                scales=w_scales[:],
                in_=w_grouped[:].rearrange("p n t -> p (n t)"),
            )

        def transpose_x(b, a, pool=ps_val, tag="val"):
            if not 0 <= b < B:
                return
            x_words = x_sb[b][:].bitcast(F32)
            xt_bank = pool.tile([P, 2, 2, P], F32, tag=tag)
            for i in range(2):
                for u in range(2):
                    nc.tensor.transpose(
                        xt_bank[:, i, u, :], x_words[:, 2 * a + i, P * u : P * (u + 1)], ident_f32[:]
                    )
            val_ps[b, a] = xt_bank

        def copy_x(b, a):
            if not 0 <= b < B:
                return
            if a == 0:
                x_grouped_tile = stage.tile([P, LT, P, PACK], BF16, align_bytes=64)
                x_grouped[b] = x_grouped_tile
            copy_out = nc.vector.tensor_copy if b == 0 and a in XV else nc.scalar.copy
            copy_out(
                out=x_grouped[b][:].bitcast(F32)[:, 2 * a : 2 * a + 2, :, :],
                in_=val_ps[b, a][:].rearrange("p i u l -> p i l u"),
            )

        def quantise_x(b):
            if not 0 <= b < B:
                return
            x_codes_tile = stage.tile([P, L], U32, align_bytes=64)
            x_scales_tile = stage.tile([P, L], U8, align_bytes=64)
            nc.vector.quantize_mx(
                out=x_codes_tile[:].bitcast(FP8X4),
                scales=x_scales_tile[:],
                in_=x_grouped[b][:].rearrange("p t l w -> p (t l w)"),
            )
            x_codes[b], x_scales[b] = x_codes_tile, x_scales_tile

        def value_matmul(b, n, pool=ps_val, tag="val"):
            if not 0 <= b < B:
                return
            v_bank = pool.tile([P, LT, KD], F32, tag=tag)
            for t in range(LT):
                nc.tensor.matmul_mx(
                    out=v_bank[:, t, :],
                    lhsT=x_codes[b][:, P * t : P * (t + 1)].bitcast(FP8X4),
                    lhsT_scale=x_scales[b][:, P * t : P * (t + 1)],
                    rhs=w_codes[:, KD * n : KD * (n + 1)].bitcast(FP8X4),
                    rhs_scale=w_scales[:, KD * n : KD * (n + 1)],
                    start=True,
                    stop=True,
                )
            val_ps[b, n] = v_bank

        def copy_v(b, n):
            if not 0 <= b < B:
                return
            if n == 0:
                v_grouped_tile = stage.tile([P, NH, KD, PACK], BF16, align_bytes=64)
                v_grouped[b] = v_grouped_tile
            copy_out = nc.vector.tensor_copy if n in VV else nc.scalar.copy
            copy_out(out=v_grouped[b][:, n, :, :], in_=val_ps[b, n][:].rearrange("p t d -> p d t"))

        def quantise_v(b):
            if not 0 <= b < B:
                return
            v_codes_tile = stage.tile([P, NH * KD], U32, align_bytes=64)
            v_scales_tile = stage.tile([P, NH * KD], U8, align_bytes=64)
            nc.vector.quantize_mx(
                out=v_codes_tile[:].bitcast(FP8X4),
                scales=v_scales_tile[:],
                in_=v_grouped[b][:].rearrange("p n d t -> p (n d t)"),
            )
            v_codes[b], v_scales[b] = v_codes_tile, v_scales_tile

        pos, qk_ps, qk_t, neg_max, row_sum, inv_sum = {}, {}, {}, {}, {}, {}
        e_grouped, e_codes, e_scales = {}, {}, {}
        sc_ps, neg_s, e_sb, et_ps = {}, {}, {}, {}

        def position_bias(g):
            if not 0 <= g < PAIRS:
                return
            pos_tile = biases.tile([P, 2, LT, GRID_H, GRID_W], F32)
            b, n = divmod(2 * g, NH)
            wanted = [k for k in range(2 * LT) if not (2 * g + k // LT in BIAS_HEADS and k % LT == BIAS_TILE)]
            runs = []
            for k in wanted:
                if runs and runs[-1][-1] == k - 1 and (g > 0 or k not in STARTS):
                    runs[-1].append(k)
                else:
                    runs.append([k])
            tiles = pos_tile[:].rearrange("p a j r c -> p (a j) r c")
            rows = rh_sb[b][:].rearrange("p n (j m) -> p (n j) m", m=RH_TILE_STEP)
            for run in runs:
                width = len(run)
                engine = nc.vector if g == 0 and run[0] in VPOS else nc.gpsimd
                engine.tensor_tensor(
                    out=tiles[:, run[0] : run[0] + width, :, :],
                    in0=rw_sb[b][:, LT * n + run[0] : LT * n + run[0] + width, :]
                    .unsqueeze(2)
                    .to_broadcast([P, width, GRID_H, GRID_W]),
                    in1=rows[:, LT * n + run[0] : LT * n + run[0] + width, 0:GRID_H]
                    .unsqueeze(3)
                    .to_broadcast([P, width, GRID_H, GRID_W]),
                    op=ALU.add,
                )
            for a in range(2):
                pos[2 * g + a] = pos_tile[:, a, :, :, :]

        terms_sb = []
        for s in range(2):
            terms_tile = const.tile([P, 2, BIAS_COLS], F32, name="terms%d" % s)
            nc.vector.memset(terms_tile[:], 0.0)
            terms_sb.append(terms_tile)
        spread = const.tile([P, 2, GRID_H, GRID_W], F32)
        terms_t = {}

        def make_spread():
            for s in range(2):
                col, row = BIAS_COLS * s, BIAS_COLS * s + GRID_W
                nc.vector.tensor_tensor(
                    out=spread[:, s, :, :],
                    in0=ident_f32[:, col : col + GRID_W].unsqueeze(1).to_broadcast([P, GRID_H, GRID_W]),
                    in1=ident_f32[:, row : row + GRID_H].unsqueeze(2).to_broadcast([P, GRID_H, GRID_W]),
                    op=ALU.add,
                )

        def bias_terms(h):
            if h not in TABLE_HEADS:
                return
            k = BIAS_HEADS.index(h)
            pair = BIAS_HEADS[k : k + 2]
            same_image = pair[0] // NH == pair[1] // NH
            for s in (0,) if same_image else (0, 1):
                b, n = divmod(pair[s], NH)
                step = pair[1] - pair[0]
                members = slice(n, n + step + 1, step) if same_image else slice(n, n + 1)
                slots = slice(0, 2) if same_image else slice(s, s + 1)
                rw_rows = rw_sb[b][:].rearrange("p (n j) c -> p n j c", j=LT)
                for in_, cols in (
                    (rw_rows[:, members, BIAS_TILE, :], slice(0, GRID_W)),
                    (
                        rh_sb[b][:, members, BIAS_TILE * RH_TILE_STEP : BIAS_TILE * RH_TILE_STEP + GRID_H],
                        slice(GRID_W, GRID_W + GRID_H),
                    ),
                ):
                    nc.scalar.mul(terms_sb[TABLE_HEADS.index(h) % 2][:, slots, cols], in_, 1.0 / SCALE)

        def transpose_terms(h, i):
            if h not in TABLE_HEADS:
                return
            if i < 0:
                et_bank = ps_et.tile([P, 4, P], F32, tag="et")
                et_ps[i] = et_bank
            nc.tensor.transpose(et_ps[i][:, 2, :], terms_sb[TABLE_HEADS.index(h) % 2][:].rearrange("p s m -> p (s m)"), ident_f32[:])

        def copy_terms(h, i):
            if h not in TABLE_HEADS:
                return
            terms_t_tile = heads.tile([P, P], F32)
            nc.scalar.copy(out=terms_t_tile[:], in_=et_ps[i][:, 2, :])
            terms_t[h] = terms_t_tile

        def transpose_qk(h):
            if not 0 <= h < HEADS:
                return
            b, n = divmod(h, NH)
            qk_bank = ps_qk.tile([P, 2, L], BF16, tag="qk")
            for j in range(LT):
                nc.tensor.transpose(qk_bank[:, 0, P * j : P * (j + 1)], q_sb[b][:, LT * n + j, :], ident_bf[:])
            for j in range(LT):
                nc.tensor.transpose(qk_bank[:, 1, P * j : P * (j + 1)], k_sb[b][:, LT * n + j, :], ident_bf[:])
            qk_ps[h] = qk_bank

        def copy_qk(h):
            if not 0 <= h < HEADS:
                return
            qk_tile = heads.tile([P, 2, L], BF16)
            nc.scalar.copy(out=qk_tile[:].bitcast(F32), in_=qk_ps[h][:].bitcast(F32))
            qk_t[h] = qk_tile

        def scores_matmul(i):
            if not 0 <= i < TILES:
                return
            h, j = divmod(i, LT)
            sc_bank = ps_sc.tile([P, L], F32, tag="sc")
            with_bias = h in BIAS_HEADS and j == BIAS_TILE
            nc.tensor.matmul(
                sc_bank[:],
                lhsT=qk_t[h][:, 0, P * j : P * (j + 1)],
                rhs=qk_t[h][:, 1, :],
                start=True,
                stop=not with_bias,
            )
            if with_bias:
                nc.tensor.matmul(
                    sc_bank[:],
                    lhsT=terms_t[TABLE_OF[h]][:],
                    rhs=spread[:, BIAS_HEADS.index(h) % 2, :, :].rearrange("p r c -> p (r c)"),
                    start=False,
                    stop=True,
                )
            sc_ps[i] = sc_bank

        def add_bias(i):
            if not 0 <= i < TILES:
                return
            h, j = divmod(i, LT)
            neg_s_tile = work.tile([P, L], F32)
            neg_s[i] = neg_s_tile
            neg_max_tile = stats.tile([P, 1], F32)
            neg_max[i] = neg_max_tile
            if h in BIAS_HEADS and j == BIAS_TILE:
                nc.vector.tensor_scalar(
                    out=neg_s_tile[:],
                    in0=sc_ps[i][:],
                    scalar1=-SCALE,
                    scalar2=None,
                    op0=ALU.mult,
                    op1=ALU.min,
                    accum_out=neg_max_tile[:],
                )
                return
            nc.vector.scalar_tensor_tensor(
                out=neg_s_tile[:],
                in0=sc_ps[i][:],
                scalar=-SCALE,
                in1=pos[h][:, j, :, :].rearrange("p r c -> p (r c)"),
                op0=ALU.mult,
                op1=ALU.subtract,
            )

        def row_minimum(i):
            if not 0 <= i < TILES:
                return
            h, j = divmod(i, LT)
            if h in BIAS_HEADS and j == BIAS_TILE:
                return
            nc.vector.tensor_reduce(
                out=neg_max[i][:], in_=neg_s[i][:], axis=mybir.AxisListType.X, op=ALU.min
            )

        def exponent(i):
            if not 0 <= i < TILES:
                return
            h, j = divmod(i, LT)
            g, k = divmod(i, 2 * LT)
            if k == 0:
                row_sum_tile = stats.tile([P, 2 * LT], F32)
                row_sum[g] = row_sum_tile
            e_tile = work.tile([P, L], BF16)
            nc.scalar.activation(
                out=e_tile[:],
                in_=neg_s[i][:],
                func=ACT.Exp,
                bias=neg_max[i][:],
                scale=-1.0,
                accum_out=row_sum[g][:, k : k + 1],
            )
            e_sb[i] = e_tile

        def transpose_e(i):
            if not 0 <= i < TILES:
                return
            e_words = e_sb[i][:].bitcast(F32)
            et_bank = ps_et.tile([P, 4, P], F32, tag="et")
            for u in range(2):
                nc.tensor.transpose(et_bank[:, u, :], e_words[:, P * u : P * (u + 1)], ident_f32[:])
            et_ps[i] = et_bank

        def copy_e(i):
            if not 0 <= i < TILES:
                return
            g, k = divmod(i, 2 * LT)
            if k == 0:
                e_grouped_tile = grouped.tile([P, 2 * LT, P, PACK], BF16, align_bytes=64)
                e_grouped[g] = e_grouped_tile
            nc.scalar.copy(out=e_grouped[g][:].bitcast(F32)[:, k, :, :], in_=et_ps[i][:, 0:2, :].rearrange("p u m -> p m u"))

        def quantise_e(g, first=0, last=2):
            if not 0 <= g < PAIRS:
                return
            if first == 0:
                inv_sum_tile = stats.tile([P, 2 * LT], F32)
                e_codes_tile = heads.tile([P, 2 * L], U32, align_bytes=64)
                e_scales_tile = heads.tile([P, 2 * L], U8, align_bytes=64)
                e_codes[g], e_scales[g], inv_sum[g] = e_codes_tile, e_scales_tile, inv_sum_tile
            tiles, cols = slice(LT * first, LT * last), slice(L * first, L * last)
            nc.vector.reciprocal(out=inv_sum[g][:, tiles], in_=row_sum[g][:, tiles])
            nc.vector.quantize_mx(
                out=e_codes[g][:, cols].bitcast(FP8X4),
                scales=e_scales[g][:, cols],
                in_=e_grouped[g][:, tiles, :, :].rearrange("p k m t -> p (k m t)"),
            )

        o_ps, o_sb = {}, {}

        def output_matmul(h, pool=ps_o, tag="o"):
            if not 0 <= h < HEADS:
                return
            b, n = divmod(h, NH)
            o_bank = pool.tile([P, LT, KD], F32, tag=tag)
            for j in range(LT):
                cols = slice(P * (LT * (h % 2) + j), P * (LT * (h % 2) + j + 1))
                nc.tensor.matmul_mx(
                    out=o_bank[:, j, :],
                    lhsT=e_codes[h // 2][:, cols].bitcast(FP8X4),
                    lhsT_scale=e_scales[h // 2][:, cols],
                    rhs=v_codes[b][:, KD * n : KD * (n + 1)].bitcast(FP8X4),
                    rhs_scale=v_scales[b][:, KD * n : KD * (n + 1)],
                    start=True,
                    stop=True,
                )
            o_ps[h] = o_bank

        def normalise(h, first, last, on_vector=False, queue=nc.sync):
            if not 0 <= h < HEADS:
                return
            b, n = divmod(h, NH)
            if first == 0:
                o_tile = outs.tile([P, LT, KD], F32)
                o_sb[h] = o_tile
            if not 0 <= h < HEADS:
                return
            factors = inv_sum[h // 2][:, LT * (h % 2) : LT * (h % 2 + 1)]
            if on_vector:
                nc.vector.tensor_tensor(
                    out=o_sb[h][:, first:last, :],
                    in0=o_ps[h][:, first:last, :],
                    in1=factors[:, first:last].unsqueeze(2).to_broadcast([P, last - first, KD]),
                    op=ALU.mult,
                )
            for j in () if on_vector else range(first, last):
                nc.scalar.activation(
                    out=o_sb[h][:, j, :], in_=o_ps[h][:, j, :], func=ACT.Copy, scale=factors[:, j : j + 1]
                )
            if last == LT:
                queue.dma_start(
                    out=out[b].rearrange("h w c -> (h w) c").rearrange("(j p) c -> p j c", p=P)[
                        :, :, KD * n : KD * (n + 1)
                    ],
                    in_=o_sb[h][:],
                )

        tensor_steps, copy_steps, quantise_steps = {}, {}, {}
        for b in range(B):
            base = LT * NH * b
            quantise_steps.setdefault(base + QV, []).append((quantise_v, b))
            if b > 0:
                quantise_steps.setdefault(base + QX, []).append((quantise_x, b))
                for a in range(2):
                    copy_steps.setdefault(base + (XC1 if b == 1 else XC)[a], []).append((copy_x, b, a))
                    tensor_steps.setdefault(base + (TX1 if b == 1 else TX)[a], []).append((transpose_x, b, a))
            for n in range(NH):
                copy_steps.setdefault((VC if b else VC0)[n] + base, []).append((copy_v, b, n))
                tensor_steps.setdefault((VM if b else VM0)[n] + base, []).append((value_matmul, b, n))

        with tc.manual_schedule():
            load_queries_and_keys(0, 0, 1)
            load_bias_tables(0, 0, 2)
            load_w()
            load_x(0)
            load_queries_and_keys(0, 1, 2)
            load_bias_tables(0, 2, NH)
            load_queries_and_keys(0, 2, NH)
            load_x(1)
            load_bias_tables(1)
            load_queries_and_keys(1)
            make_spread()
            position_bias(0)
            transpose_qk(0)
            copy_qk(0)
            for i in range(3):
                scores_matmul(i)
            add_bias(0)
            row_minimum(0)
            copy_w()
            transpose_x(0, 0)
            transpose_x(0, 1, ps_o, "o")
            copy_x(0, 0)
            copy_x(0, 1)
            exponent(0)
            scores_matmul(3)
            for i in range(1, 4):
                add_bias(i)
                row_minimum(i)
            quantise_w()
            quantise_x(0)
            for i in range(-8, TILES):
                h, j = divmod(i, LT)
                g, step = divmod(i - 4, 2 * LT)
                if i >= 0 and i % (NH * LT) == 0:
                    load_x(h // NH + 2)
                    load_bias_tables(h // NH + 2)
                    load_queries_and_keys(h // NH + 2)
                if i + SC > 3:
                    scores_matmul(i + SC)
                for stage_of, b, part in tensor_steps.get(i, ()):
                    if EARLY and part in VV and stage_of is value_matmul:
                        stage_of(b, part)
                if i + AD > 3:
                    add_bias(i + AD)
                if step == 0 and i < TILES - LT:
                    quantise_e(g - 1)
                    for stage_of, b in quantise_steps.get(i, ()):
                        stage_of(b)
                    if g + 2 > 0:
                        position_bias(g + 2)
                    if (2 * g - 3) % NH in NV and 2 * g - 3 < HEADS - 4:
                        normalise(2 * g - 3, 0, LT, True)
                if j == 0:
                    bias_terms(h + 3)
                if i + MN > 3:
                    row_minimum(i + MN)
                for stage_of, b, part in copy_steps.get(i, ()):
                    if part in VV and stage_of is copy_v:
                        stage_of(b, part)
                if i > 0:
                    exponent(i)
                transpose_e(i - TE)
                copy_e(i - CE)
                if j == QKC and h > -2:
                    copy_qk(h + 2)
                if j == TM + 1:
                    copy_terms(h + 3, i - 2)
                for a in range(2):
                    if g < PAIRS - 1 and (2 * (g - 1) + a) % NH not in NV:
                        if step == NM + LT * a:
                            normalise(2 * (g - 1) + a, 0, LT // 2)
                        if step == NM + 1 + LT * a:
                            normalise(2 * (g - 1) + a, LT // 2, LT)
                for stage_of, b, part in copy_steps.get(i, ()):
                    if part not in VV or stage_of is copy_x:
                        stage_of(b, part)
                if j == QKT and h + (QKT == 3) > -2:
                    transpose_qk(h + 2 + (QKT == 3))
                if j == TM:
                    transpose_terms(h + 3, i - 1)
                for a in range(2):
                    if step == OM + LT * a and g < PAIRS - 1:
                        output_matmul(2 * (g - 1) + a)
                for stage_of, b, part in tensor_steps.get(i, ()):
                    if not EARLY or part not in VV or stage_of is transpose_x:
                        stage_of(b, part)
            transpose_e(TILES - 1)
            copy_e(TILES - 2)
            copy_e(TILES - 1)
            quantise_e(PAIRS - 2)
            quantise_v(B - 1)
            quantise_e(PAIRS - 1, 0, 1)
            for a in range(3):
                output_matmul(HEADS - 4 + a, ps_sc, "sc")
            quantise_e(PAIRS - 1, 1, 2)
            output_matmul(HEADS - 1)
            normalise(HEADS - 4, 0, LT, True)
            normalise(HEADS - 3, 0, LT, False, nc.scalar)
            normalise(HEADS - 2, 0, LT, False, nc.scalar)
            normalise(HEADS - 1, 0, LT, True)
